import numpy as np
import ml_dtypes


def mxq(x, axis, fmt="e4m3"):
    dtype, down = {"e4m3": (ml_dtypes.float8_e4m3fn, 7), "e5m2": (ml_dtypes.float8_e5m2, 14)}[fmt]
    v = np.moveaxis(np.asarray(x, np.float32).astype(ml_dtypes.bfloat16).astype(np.float64), axis, -1)
    blocks = v.reshape(v.shape[:-1] + (-1, 32))
    amax = np.abs(blocks).max(-1, keepdims=True)
    byte = np.maximum(np.where(amax > 0, np.frexp(amax)[1] - 1 + 127, 0) - down, 1)
    scale = np.exp2(byte - 127.0)
    codes = (blocks / scale).astype(np.float32).astype(dtype).astype(np.float64)
    return np.moveaxis((codes * scale).reshape(v.shape), -1, axis)


WIDE = False


def mx_kscale(k):
    if not WIDE:
        return np.ones(k)
    levels = np.array([10, -10, 5, -5, 0])
    a = np.random.permutation(np.resize(levels, k // 512 * 4)).reshape(k // 512, 4)
    idx = np.arange(k)
    return np.exp2(a[idx // 512, idx % 128 // 32])


BF16 = ml_dtypes.bfloat16


def bf(x):
    return np.asarray(x, np.float32).astype(BF16)


def f64(x):
    return np.asarray(x).astype(np.float64)


B, H, S, D, W = 1, 2, 2048, 128, 256
HALF = W // 2
QB = W
KB = 2 * W
NB = S // QB
START = np.clip(np.arange(NB) * QB - HALF, 0, S - KB)
ROW = (np.arange(NB)[:, None] * QB + np.arange(QB))[:, :, None]
COL = (START[:, None] + np.arange(KB))[:, None, :]
MASK = (COL >= ROW - HALF) & (COL < ROW + HALF)


def setup_inputs():
    shape = (B, H, S, D)
    s = mx_kscale(S)
    top = np.array([s[max(i - HALF, 0):i + HALF].max() for i in range(S)])
    c = np.array([top[max(j - HALF + 1, 0):j + HALF + 1].min() for j in range(S)])
    q = np.random.standard_normal(shape) * 1.5
    k = np.random.standard_normal(shape)
    v = np.random.standard_normal(shape) * 2.0
    q[..., 0] = 4.0
    k[..., 0] += np.log(s) * D ** 0.5 / 4.0
    v = v * (c / s)[:, None]
    return {"q": bf(q), "k": bf(k), "v": bf(v)}


def reference(q, k, v):
    q, k = f64(q), f64(k)
    vq = mxq(f64(v), 2, "e4m3")
    scale = 1.0 / (D ** 0.5)
    qb = q.reshape(B, H, NB, QB, D)
    kb = np.stack([k[:, :, c:c + KB] for c in START], 2)
    vb = np.stack([vq[:, :, c:c + KB] for c in START], 2)
    s = qb @ kb.transpose(0, 1, 2, 4, 3) * scale
    s = np.where(MASK, s, -np.inf)
    e = np.exp(s - s.max(-1, keepdims=True))
    out = (mxq(e, 4, "e4m3") @ vb) / e.sum(-1, keepdims=True)
    return out.reshape(B, H, S, D)

@@ -1,0 +1,216 @@
+from contextlib import ExitStack
+
+import concourse.mybir as mybir
+from concourse.masks import make_identity
+
+BF16 = mybir.dt.bfloat16
+F32 = mybir.dt.float32
+U32 = mybir.dt.uint32
+U8 = mybir.dt.uint8
+FP8X4 = mybir.dt.float8_e4m3fn_x4
+ALU = mybir.AluOpType
+ACT = mybir.ActivationFunctionType
+AXIS = mybir.AxisListType
+
+P = 128
+PACK = 4
+HEADS = 2
+SEQ = 2048
+DIM = 128
+HALF = 128
+SPAN = P * PACK
+Q_TILE = P
+TILES = SEQ // Q_TILE
+PAIRS = TILES // 2
+LIVE = Q_TILE + 2 * HALF
+LIVE_X = LIVE // PACK
+GROUP = 4
+SCALE = 1.0 / DIM**0.5
+MASKED = -1.0e30
+
+FLOPS = 2 * 2 * HEADS * SEQ * SPAN * DIM
+
+
+def span_start(pair):
+    return min(max(2 * Q_TILE * pair - HALF, 0), SEQ - SPAN)
+
+
+def first_live_key(t_idx):
+    return min(max(Q_TILE * t_idx - HALF, 0), SEQ - LIVE)
+
+
+def tile_sparseattention_kernel(tc, q, k, v, out):
+    nc = tc.nc
+    q_rows = q.rearrange("b h s d -> (b h s) d")
+    k_rows = k.rearrange("b h s d -> (b h s) d")
+    v_rows = v.rearrange("b h s d -> (b h s) d")
+    out_rows = out.rearrange("b h s d -> (b h s) d")
+
+    with ExitStack() as ctx:
+        keep = ctx.enter_context(tc.tile_pool(name="keep", bufs=1))
+        work = ctx.enter_context(tc.tile_pool(name="work", bufs=3))
+        small = ctx.enter_context(tc.tile_pool(name="small", bufs=6))
+        psum = ctx.enter_context(tc.psum_pool(name="psum", bufs=2))
+
+        k_raw = keep.tile([P, HEADS, SEQ // SPAN, PACK, DIM], BF16)
+        q_raw = keep.tile([P, HEADS, TILES, DIM], BF16)
+        v_raw = keep.tile([P, HEADS, PAIRS, PACK, DIM], BF16)
+        for h in range(HEADS):
+            rows = slice(h * SEQ, (h + 1) * SEQ)
+            nc.sync.dma_start(
+                out=k_raw[:, h].rearrange("p a t d -> p a (t d)"),
+                in_=k_rows[rows, :].rearrange("(a p t) d -> p a (t d)", p=P, t=PACK),
+            )
+            nc.sync.dma_start(
+                out=q_raw[:, h], in_=q_rows[rows, :].rearrange("(n p) d -> p n d", p=P)
+            )
+            for pair in range(PAIRS):
+                c = h * SEQ + span_start(pair)
+                nc.sync.dma_start(
+                    out=v_raw[:, h, pair].rearrange("p t d -> p (t d)"),
+                    in_=v_rows[c : c + SPAN, :].rearrange("(p t) d -> p (t d)", t=PACK),
+                )
+
+        ident = keep.tile([P, P], BF16)
+        make_identity(nc, ident[:])
+
+        mask_of = {}
+        for lo in (-HALF, 0, HALF):
+            mask = keep.tile([P, PACK, LIVE_X], F32, name="mask%d" % (lo + HALF))
+            nc.gpsimd.memset(mask[:], 0.0)
+            nc.gpsimd.affine_select(
+                out=mask[:], in_=mask[:], pattern=[[1, PACK], [PACK, LIVE_X]],
+                compare_op=ALU.is_ge, fill=MASKED, base=-lo, channel_multiplier=-1,
+            )
+            nc.gpsimd.affine_select(
+                out=mask[:], in_=mask[:], pattern=[[-1, PACK], [-PACK, LIVE_X]],
+                compare_op=ALU.is_ge, fill=MASKED, base=lo + 2 * HALF - 1, channel_multiplier=1,
+            )
+            mask_of[lo] = mask
+
+        E_BUFS = 2
+        e_tiles = {}
+        e_uses = {0: 0, P - LIVE_X: 0}
+        for x_lo in (0, P - LIVE_X):
+            for b in range(E_BUFS):
+                e_tile = keep.tile([P, PACK, P], BF16, name="e%d_%d" % (x_lo, b))
+                nc.vector.memset(e_tile[:], 0.0)
+                e_tiles[(x_lo, b)] = e_tile
+
+        kT = keep.tile([P, HEADS, PACK, SEQ // PACK], BF16)
+        qT = keep.tile([P, HEADS, SEQ], BF16)
+
+        def transpose_chunk(h, a):
+            k_ps = psum.tile([P, PACK, P], BF16, tag="tp")
+            for t in range(PACK):
+                nc.tensor.transpose(k_ps[:, t, :], k_raw[:, h, a, t, :], ident[:])
+            nc.vector.tensor_copy(out=kT[:, h, :, a * P : (a + 1) * P], in_=k_ps[:])
+            q_ps = psum.tile([P, PACK, P], BF16, tag="tp")
+            for t in range(PACK):
+                nc.tensor.transpose(q_ps[:, t, :], q_raw[:, h, PACK * a + t, :], ident[:])
+            nc.scalar.copy(
+                out=qT[:, h, a * SPAN : (a + 1) * SPAN],
+                in_=q_ps[:].rearrange("p t i -> p (t i)"),
+            )
+
+        v_codes = keep.tile([P, HEADS, PAIRS, DIM], U32, align_bytes=64)
+        v_scales = keep.tile([P, HEADS, PAIRS, DIM], U8, align_bytes=64)
+        V_BATCH = 4
+
+        def quantise_v(h, first):
+            spans = slice(first, first + V_BATCH)
+            v_grouped = work.tile([P, V_BATCH, DIM, PACK], BF16, align_bytes=64)
+            nc.vector.tensor_copy(
+                out=v_grouped[:], in_=v_raw[:, h, spans].rearrange("p n t d -> p n d t")
+            )
+            nc.vector.quantize_mx(
+                out=v_codes[:, h, spans, :].rearrange("p n d -> p (n d)").bitcast(FP8X4),
+                scales=v_scales[:, h, spans, :].rearrange("p n d -> p (n d)"),
+                in_=v_grouped[:].rearrange("p n d t -> p (n d t)"),
+            )
+
+        def scores_and_exp(h, t_idx, e_sum):
+            key0 = first_live_key(t_idx)
+            x_lo = (key0 - span_start(t_idx // 2)) // PACK
+            s_ps = psum.tile([P, PACK, LIVE_X], F32, tag="s")
+            nc.tensor.matmul(
+                s_ps[:],
+                lhsT=qT[:, h, t_idx * Q_TILE : (t_idx + 1) * Q_TILE],
+                rhs=kT[:, h, :, key0 // PACK : key0 // PACK + LIVE_X],
+                start=True,
+                stop=True,
+            )
+            mask = mask_of[Q_TILE * t_idx - HALF - key0]
+            s_masked = work.tile([P, PACK, LIVE_X], F32)
+            nc.vector.scalar_tensor_tensor(
+                out=s_masked[:], in0=s_ps[:], scalar=SCALE, in1=mask[:],
+                op0=ALU.mult, op1=ALU.add,
+            )
+            neg_max = small.tile([P, 1], F32)
+            nc.vector.tensor_reduce(
+                out=neg_max[:], in_=s_masked[:].rearrange("p t x -> p (t x)"),
+                axis=AXIS.X, op=ALU.max, negate=True,
+            )
+            e_tile = e_tiles[(x_lo, e_uses[x_lo] % E_BUFS)]
+            e_uses[x_lo] += 1
+            nc.scalar.activation(
+                out=e_tile[:, :, x_lo : x_lo + LIVE_X], in_=s_masked[:], func=ACT.Exp,
+                bias=neg_max[:], scale=1.0, accum_out=e_sum,
+            )
+            return e_tile
+
+        for a in range(SEQ // SPAN):
+            transpose_chunk(0, a)
+        quantise_v(0, 0)
+
+        for h in range(HEADS):
+            for first_pair in range(0, PAIRS, GROUP // 2):
+                o_ps = psum.tile([P, GROUP, DIM], F32, tag="o")
+                e_sums = small.tile([P, GROUP], F32)
+                for pair in (first_pair, first_pair + 1):
+                    eT_ps = psum.tile([P, 2, PACK, Q_TILE], BF16, tag="eT")
+                    for j in range(2):
+                        g = 2 * (pair - first_pair) + j
+                        e_tile = scores_and_exp(h, 2 * pair + j, e_sums[:, g : g + 1])
+                        for t in range(PACK):
+                            nc.tensor.transpose(eT_ps[:, j, t, :], e_tile[:, t, :], ident[:])
+                    e_grouped = work.tile([P, 2, Q_TILE, PACK], BF16, align_bytes=64)
+                    nc.scalar.copy(out=e_grouped[:], in_=eT_ps[:].rearrange("p j t i -> p j i t"))
+                    e_codes = work.tile([P, 2 * Q_TILE], U32, align_bytes=64)
+                    e_scales = work.tile([P, 2 * Q_TILE], U8, align_bytes=64)
+                    nc.vector.quantize_mx(
+                        out=e_codes[:].bitcast(FP8X4),
+                        scales=e_scales[:],
+                        in_=e_grouped[:].rearrange("p j i t -> p (j i t)"),
+                    )
+                    for j in range(2):
+                        g = 2 * (pair - first_pair) + j
+                        cols = slice(j * Q_TILE, (j + 1) * Q_TILE)
+                        nc.tensor.matmul_mx(
+                            out=o_ps[:, g, :],
+                            lhsT=e_codes[:, cols].bitcast(FP8X4),
+                            lhsT_scale=e_scales[:, cols],
+                            rhs=v_codes[:, h, pair, :].bitcast(FP8X4),
+                            rhs_scale=v_scales[:, h, pair, :],
+                            start=True,
+                            stop=True,
+                        )
+                r_sums = small.tile([P, GROUP], F32)
+                nc.vector.reciprocal(out=r_sums[:], in_=e_sums[:])
+                o_sb = work.tile([P, GROUP, DIM], F32)
+                nc.vector.tensor_tensor(
+                    out=o_sb[:], in0=o_ps[:],
+                    in1=r_sums[:].unsqueeze(2).to_broadcast([P, GROUP, DIM]), op=ALU.mult,
+                )
+                row0 = h * SEQ + 2 * first_pair * Q_TILE
+                nc.sync.dma_start(
+                    out=out_rows[row0 : row0 + GROUP * Q_TILE, :].rearrange("(g p) d -> p g d", p=P),
+                    in_=o_sb[:],
+                )
+                step = first_pair // (GROUP // 2)
+                if step == 0:
+                    quantise_v(h, V_BATCH)
+                if h + 1 < HEADS:
+                    transpose_chunk(h + 1, step)
+                    if step == 2:
+                        quantise_v(h + 1, 0)

@@ -22,8 +22,11 @@ SPAN = P * PACK
 Q_TILE = P
 TILES = SEQ // Q_TILE
 PAIRS = TILES // 2
-LIVE = Q_TILE + 2 * HALF
-LIVE_X = LIVE // PACK
+N_PAIRS = HEADS * PAIRS
+CHUNKS = SEQ // SPAN
+STEPS_AHEAD = 3
+BLOCK = 128
+BLOCK_X = BLOCK // PACK
 GROUP = 4
 SCALE = 1.0 / DIM**0.5
 MASKED = -1.0e30
@@ -35,8 +38,8 @@ def span_start(pair):
     return min(max(2 * Q_TILE * pair - HALF, 0), SEQ - SPAN)
 
 
-def first_live_key(t_idx):
-    return min(max(Q_TILE * t_idx - HALF, 0), SEQ - LIVE)
+def key_blocks(t_idx):
+    return [b for b in (t_idx - 1, t_idx, t_idx + 1) if 0 <= b < TILES]
 
 
 def tile_sparseattention_kernel(tc, q, k, v, out):
@@ -49,168 +52,236 @@ def tile_sparseattention_kernel(tc, q, k, v, out):
     with ExitStack() as ctx:
         keep = ctx.enter_context(tc.tile_pool(name="keep", bufs=1))
         work = ctx.enter_context(tc.tile_pool(name="work", bufs=3))
-        small = ctx.enter_context(tc.tile_pool(name="small", bufs=6))
-        psum = ctx.enter_context(tc.psum_pool(name="psum", bufs=2))
+        small = ctx.enter_context(tc.tile_pool(name="small", bufs=4))
+        psum_s = ctx.enter_context(tc.psum_pool(name="psum_s", bufs=4))
+        psum_2 = ctx.enter_context(tc.psum_pool(name="psum_2", bufs=2))
+        psum_1 = ctx.enter_context(tc.psum_pool(name="psum_1", bufs=1))
+        ctx.enter_context(tc.manual_schedule())
 
-        k_raw = keep.tile([P, HEADS, SEQ // SPAN, PACK, DIM], BF16)
-        q_raw = keep.tile([P, HEADS, TILES, DIM], BF16)
-        v_raw = keep.tile([P, HEADS, PAIRS, PACK, DIM], BF16)
-        for h in range(HEADS):
-            rows = slice(h * SEQ, (h + 1) * SEQ)
-            nc.sync.dma_start(
-                out=k_raw[:, h].rearrange("p a t d -> p a (t d)"),
-                in_=k_rows[rows, :].rearrange("(a p t) d -> p a (t d)", p=P, t=PACK),
-            )
-            nc.sync.dma_start(
-                out=q_raw[:, h], in_=q_rows[rows, :].rearrange("(n p) d -> p n d", p=P)
-            )
-            for pair in range(PAIRS):
-                c = h * SEQ + span_start(pair)
+        k_raw = keep.tile([P, HEADS, CHUNKS, PACK, DIM], BF16)
+        q_raw = keep.tile([P, HEADS, CHUNKS, PACK, DIM], BF16)
+        v_raw = keep.tile([P, N_PAIRS, PACK, DIM], BF16)
+        for n in range(N_PAIRS):
+            h, a = n // (2 * CHUNKS), (n // 2) % CHUNKS
+            rows = slice(h * SEQ + a * SPAN, h * SEQ + (a + 1) * SPAN)
+            if n % 2 == 0:
                 nc.sync.dma_start(
-                    out=v_raw[:, h, pair].rearrange("p t d -> p (t d)"),
-                    in_=v_rows[c : c + SPAN, :].rearrange("(p t) d -> p (t d)", t=PACK),
+                    out=k_raw[:, h, a].rearrange("p t d -> p (t d)"),
+                    in_=k_rows[rows, :].rearrange("(p t) d -> p (t d)", t=PACK),
                 )
+            else:
+                nc.sync.dma_start(
+                    out=q_raw[:, h, a], in_=q_rows[rows, :].rearrange("(n p) d -> p n d", p=P)
+                )
+            c = (n // PAIRS) * SEQ + span_start(n % PAIRS)
+            nc.sync.dma_start(
+                out=v_raw[:, n].rearrange("p t d -> p (t d)"),
+                in_=v_rows[c : c + SPAN, :].rearrange("(p t) d -> p (t d)", t=PACK),
+            )
 
         ident = keep.tile([P, P], BF16)
         make_identity(nc, ident[:])
-
-        mask_of = {}
-        for lo in (-HALF, 0, HALF):
-            mask = keep.tile([P, PACK, LIVE_X], F32, name="mask%d" % (lo + HALF))
-            nc.gpsimd.memset(mask[:], 0.0)
-            nc.gpsimd.affine_select(
-                out=mask[:], in_=mask[:], pattern=[[1, PACK], [PACK, LIVE_X]],
-                compare_op=ALU.is_ge, fill=MASKED, base=-lo, channel_multiplier=-1,
-            )
-            nc.gpsimd.affine_select(
-                out=mask[:], in_=mask[:], pattern=[[-1, PACK], [-PACK, LIVE_X]],
-                compare_op=ALU.is_ge, fill=MASKED, base=lo + 2 * HALF - 1, channel_multiplier=1,
-            )
-            mask_of[lo] = mask
+        ident_f32 = keep.tile([P, P], F32)
+        make_identity(nc, ident_f32[:])
 
         E_BUFS = 2
         e_tiles = {}
-        e_uses = {0: 0, P - LIVE_X: 0}
-        for x_lo in (0, P - LIVE_X):
+        e_uses = {}
+        for case in ((0, 2), (0, 3), (BLOCK_X, 3), (2 * BLOCK_X, 2)):
+            e_uses[case] = 0
             for b in range(E_BUFS):
-                e_tile = keep.tile([P, PACK, P], BF16, name="e%d_%d" % (x_lo, b))
+                e_tile = keep.tile([P, PACK, P], BF16, name="e%d_%d_%d" % (case[0], case[1], b))
                 nc.vector.memset(e_tile[:], 0.0)
-                e_tiles[(x_lo, b)] = e_tile
+                e_tiles[(case, b)] = e_tile
 
-        kT = keep.tile([P, HEADS, PACK, SEQ // PACK], BF16)
+        kT = keep.tile([P, HEADS, TILES, PACK, BLOCK_X], BF16)
         qT = keep.tile([P, HEADS, SEQ], BF16)
 
-        def transpose_chunk(h, a):
-            k_ps = psum.tile([P, PACK, P], BF16, tag="tp")
+        def transpose_step(n):
+            h, a = n // (2 * CHUNKS), (n // 2) % CHUNKS
+            raw = k_raw if n % 2 == 0 else q_raw
+            if n < STEPS_AHEAD - 1:
+                t_ps = psum_2.tile([P, PACK, P], BF16, tag="eT")
+            else:
+                t_ps = psum_1.tile([P, PACK, P], BF16, tag="tp")
             for t in range(PACK):
-                nc.tensor.transpose(k_ps[:, t, :], k_raw[:, h, a, t, :], ident[:])
-            nc.vector.tensor_copy(out=kT[:, h, :, a * P : (a + 1) * P], in_=k_ps[:])
-            q_ps = psum.tile([P, PACK, P], BF16, tag="tp")
-            for t in range(PACK):
-                nc.tensor.transpose(q_ps[:, t, :], q_raw[:, h, PACK * a + t, :], ident[:])
-            nc.scalar.copy(
-                out=qT[:, h, a * SPAN : (a + 1) * SPAN],
-                in_=q_ps[:].rearrange("p t i -> p (t i)"),
-            )
+                nc.tensor.transpose(t_ps[:, t, :], raw[:, h, a, t, :], ident[:])
+            if n % 2 == 0:
+                nc.vector.tensor_copy(
+                    out=kT[:, h, PACK * a : PACK * (a + 1)].rearrange("p b t x -> p t b x"),
+                    in_=t_ps[:].rearrange("p t (b x) -> p t b x", x=BLOCK_X),
+                )
+            else:
+                nc.scalar.copy(
+                    out=qT[:, h, a * SPAN : (a + 1) * SPAN],
+                    in_=t_ps[:].rearrange("p t i -> p (t i)"),
+                )
 
-        v_codes = keep.tile([P, HEADS, PAIRS, DIM], U32, align_bytes=64)
-        v_scales = keep.tile([P, HEADS, PAIRS, DIM], U8, align_bytes=64)
-        V_BATCH = 4
+        v_codes = keep.tile([P, N_PAIRS, DIM], U32, align_bytes=64)
+        v_scales = keep.tile([P, N_PAIRS, DIM], U8, align_bytes=64)
+        live = {}
 
-        def quantise_v(h, first):
-            spans = slice(first, first + V_BATCH)
-            v_grouped = work.tile([P, V_BATCH, DIM, PACK], BF16, align_bytes=64)
-            nc.vector.tensor_copy(
-                out=v_grouped[:], in_=v_raw[:, h, spans].rearrange("p n t d -> p n d t")
-            )
+        def regroup_v(n):
+            v_grouped = work.tile([P, DIM, PACK], BF16, align_bytes=64)
+            nc.vector.tensor_copy(out=v_grouped[:], in_=v_raw[:, n].rearrange("p t d -> p d t"))
+            live[("v", n)] = v_grouped
+
+        def quantise_v(n):
             nc.vector.quantize_mx(
-                out=v_codes[:, h, spans, :].rearrange("p n d -> p (n d)").bitcast(FP8X4),
-                scales=v_scales[:, h, spans, :].rearrange("p n d -> p (n d)"),
-                in_=v_grouped[:].rearrange("p n d t -> p (n d t)"),
+                out=v_codes[:, n, :].bitcast(FP8X4),
+                scales=v_scales[:, n, :],
+                in_=live[("v", n)][:].rearrange("p d t -> p (d t)"),
             )
 
-        def scores_and_exp(h, t_idx, e_sum):
-            key0 = first_live_key(t_idx)
-            x_lo = (key0 - span_start(t_idx // 2)) // PACK
-            s_ps = psum.tile([P, PACK, LIVE_X], F32, tag="s")
-            nc.tensor.matmul(
-                s_ps[:],
-                lhsT=qT[:, h, t_idx * Q_TILE : (t_idx + 1) * Q_TILE],
-                rhs=kT[:, h, :, key0 // PACK : key0 // PACK + LIVE_X],
-                start=True,
-                stop=True,
-            )
-            mask = mask_of[Q_TILE * t_idx - HALF - key0]
-            s_masked = work.tile([P, PACK, LIVE_X], F32)
-            nc.vector.scalar_tensor_tensor(
-                out=s_masked[:], in0=s_ps[:], scalar=SCALE, in1=mask[:],
-                op0=ALU.mult, op1=ALU.add,
-            )
+        def scores(n, j):
+            h, t_idx = n // PAIRS, 2 * (n % PAIRS) + j
+            s_ps = psum_s.tile([P, 3, PACK, BLOCK_X], F32, tag="s")
+            for g, b in enumerate(key_blocks(t_idx)):
+                if b != t_idx:
+                    nc.tensor.matmul(
+                        s_ps[:, g].rearrange("p t x -> p (t x)"),
+                        lhsT=triT[:, 0 if b < t_idx else 1, :],
+                        rhs=ident_f32[:],
+                        is_transpose=True,
+                        start=True,
+                        stop=False,
+                    )
+                nc.tensor.matmul(
+                    s_ps[:, g].rearrange("p t x -> p (t x)"),
+                    lhsT=qT[:, h, t_idx * Q_TILE : (t_idx + 1) * Q_TILE],
+                    rhs=kT[:, h, b].rearrange("p t x -> p (t x)"),
+                    start=(b == t_idx),
+                    stop=True,
+                )
+            live[("s", n, j)] = s_ps
+
+        def row_max(n, j):
+            n_blocks = len(key_blocks(2 * (n % PAIRS) + j))
             neg_max = small.tile([P, 1], F32)
             nc.vector.tensor_reduce(
-                out=neg_max[:], in_=s_masked[:].rearrange("p t x -> p (t x)"),
+                out=neg_max[:],
+                in_=live[("s", n, j)][:, :n_blocks].rearrange("p g t x -> p (g t x)"),
                 axis=AXIS.X, op=ALU.max, negate=True,
             )
-            e_tile = e_tiles[(x_lo, e_uses[x_lo] % E_BUFS)]
-            e_uses[x_lo] += 1
-            nc.scalar.activation(
-                out=e_tile[:, :, x_lo : x_lo + LIVE_X], in_=s_masked[:], func=ACT.Exp,
-                bias=neg_max[:], scale=1.0, accum_out=e_sum,
-            )
-            return e_tile
+            bias = small.tile([P, 1], F32)
+            nc.vector.tensor_scalar_mul(out=bias[:], in0=neg_max[:], scalar1=SCALE)
+            live[("bias", n, j)] = bias
 
-        for a in range(SEQ // SPAN):
-            transpose_chunk(0, a)
-        quantise_v(0, 0)
-
-        for h in range(HEADS):
-            for first_pair in range(0, PAIRS, GROUP // 2):
-                o_ps = psum.tile([P, GROUP, DIM], F32, tag="o")
+        def exponentials(n, j):
+            t_idx = 2 * (n % PAIRS) + j
+            blocks = key_blocks(t_idx)
+            x_lo = (BLOCK * blocks[0] - span_start(n % PAIRS)) // PACK
+            case = (x_lo, len(blocks))
+            e_tile = e_tiles[(case, e_uses[case] % E_BUFS)]
+            e_uses[case] += 1
+            if n % 2 == 0 and j == 0:
                 e_sums = small.tile([P, GROUP], F32)
-                for pair in (first_pair, first_pair + 1):
-                    eT_ps = psum.tile([P, 2, PACK, Q_TILE], BF16, tag="eT")
-                    for j in range(2):
-                        g = 2 * (pair - first_pair) + j
-                        e_tile = scores_and_exp(h, 2 * pair + j, e_sums[:, g : g + 1])
-                        for t in range(PACK):
-                            nc.tensor.transpose(eT_ps[:, j, t, :], e_tile[:, t, :], ident[:])
-                    e_grouped = work.tile([P, 2, Q_TILE, PACK], BF16, align_bytes=64)
-                    nc.scalar.copy(out=e_grouped[:], in_=eT_ps[:].rearrange("p j t i -> p j i t"))
-                    e_codes = work.tile([P, 2 * Q_TILE], U32, align_bytes=64)
-                    e_scales = work.tile([P, 2 * Q_TILE], U8, align_bytes=64)
-                    nc.vector.quantize_mx(
-                        out=e_codes[:].bitcast(FP8X4),
-                        scales=e_scales[:],
-                        in_=e_grouped[:].rearrange("p j i t -> p (j i t)"),
-                    )
-                    for j in range(2):
-                        g = 2 * (pair - first_pair) + j
-                        cols = slice(j * Q_TILE, (j + 1) * Q_TILE)
-                        nc.tensor.matmul_mx(
-                            out=o_ps[:, g, :],
-                            lhsT=e_codes[:, cols].bitcast(FP8X4),
-                            lhsT_scale=e_scales[:, cols],
-                            rhs=v_codes[:, h, pair, :].bitcast(FP8X4),
-                            rhs_scale=v_scales[:, h, pair, :],
-                            start=True,
-                            stop=True,
-                        )
-                r_sums = small.tile([P, GROUP], F32)
-                nc.vector.reciprocal(out=r_sums[:], in_=e_sums[:])
-                o_sb = work.tile([P, GROUP, DIM], F32)
-                nc.vector.tensor_tensor(
-                    out=o_sb[:], in0=o_ps[:],
-                    in1=r_sums[:].unsqueeze(2).to_broadcast([P, GROUP, DIM]), op=ALU.mult,
+                live[("sums", n // 2)] = e_sums
+            g = 2 * (n % 2) + j
+            nc.scalar.activation(
+                out=e_tile[:, :, x_lo : x_lo + len(blocks) * BLOCK_X].rearrange(
+                    "p t (g x) -> p g t x", x=BLOCK_X
+                ),
+                in_=live[("s", n, j)][:, : len(blocks)],
+                func=ACT.Exp, bias=live[("bias", n, j)][:], scale=SCALE,
+                accum_out=live[("sums", n // 2)][:, g : g + 1],
+            )
+            live[("e", n, j)] = e_tile
+
+        def transpose_e(n):
+            eT_ps = psum_2.tile([P, 2, PACK, Q_TILE], BF16, tag="eT")
+            for j in range(2):
+                for t in range(PACK):
+                    nc.tensor.transpose(eT_ps[:, j, t, :], live[("e", n, j)][:, t, :], ident[:])
+            live[("eT", n)] = eT_ps
+
+        def regroup_e(n):
+            e_grouped = work.tile([P, 2, Q_TILE, PACK], BF16, align_bytes=64)
+            nc.scalar.copy(
+                out=e_grouped[:], in_=live[("eT", n)][:].rearrange("p j t i -> p j i t")
+            )
+            live[("eg", n)] = e_grouped
+
+        def weighted_sum(n):
+            e_codes = work.tile([P, 2 * Q_TILE], U32, align_bytes=64)
+            e_scales = work.tile([P, 2 * Q_TILE], U8, align_bytes=64)
+            nc.vector.quantize_mx(
+                out=e_codes[:].bitcast(FP8X4),
+                scales=e_scales[:],
+                in_=live[("eg", n)][:].rearrange("p j i t -> p (j i t)"),
+            )
+            if n % 2 == 0:
+                o_ps = psum_1.tile([P, GROUP, DIM], F32, tag="o")
+                live[("o", n // 2)] = o_ps
+            for j in range(2):
+                cols = slice(j * Q_TILE, (j + 1) * Q_TILE)
+                nc.tensor.matmul_mx(
+                    out=live[("o", n // 2)][:, 2 * (n % 2) + j, :],
+                    lhsT=e_codes[:, cols].bitcast(FP8X4),
+                    lhsT_scale=e_scales[:, cols],
+                    rhs=v_codes[:, n, :].bitcast(FP8X4),
+                    rhs_scale=v_scales[:, n, :],
+                    start=True,
+                    stop=True,
                 )
-                row0 = h * SEQ + 2 * first_pair * Q_TILE
-                nc.sync.dma_start(
-                    out=out_rows[row0 : row0 + GROUP * Q_TILE, :].rearrange("(g p) d -> p g d", p=P),
-                    in_=o_sb[:],
-                )
-                step = first_pair // (GROUP // 2)
-                if step == 0:
-                    quantise_v(h, V_BATCH)
-                if h + 1 < HEADS:
-                    transpose_chunk(h + 1, step)
-                    if step == 2:
-                        quantise_v(h + 1, 0)
+
+        def finish(group):
+            r_sums = small.tile([P, GROUP], F32)
+            nc.vector.reciprocal(out=r_sums[:], in_=live[("sums", group)][:])
+            o_sb = work.tile([P, GROUP, DIM], F32)
+            nc.vector.tensor_tensor(
+                out=o_sb[:], in0=live[("o", group)][:],
+                in1=r_sums[:].unsqueeze(2).to_broadcast([P, GROUP, DIM]), op=ALU.mult,
+            )
+            row0 = group * GROUP * Q_TILE
+            nc.sync.dma_start(
+                out=out_rows[row0 : row0 + GROUP * Q_TILE, :].rearrange("(g p) d -> p g d", p=P),
+                in_=o_sb[:],
+            )
+
+        for n in range(STEPS_AHEAD - 1):
+            transpose_step(n)
+
+        tri = keep.tile([P, 2, PACK, BLOCK_X], F32)
+        nc.gpsimd.memset(tri[:], 0.0)
+        nc.gpsimd.affine_select(
+            out=tri[:, 0], in_=tri[:, 0], pattern=[[1, PACK], [PACK, BLOCK_X]],
+            compare_op=ALU.is_ge, fill=MASKED, base=0, channel_multiplier=-1,
+        )
+        nc.gpsimd.affine_select(
+            out=tri[:, 1], in_=tri[:, 1], pattern=[[-1, PACK], [-PACK, BLOCK_X]],
+            compare_op=ALU.is_ge, fill=MASKED, base=-1, channel_multiplier=1,
+        )
+        triT_ps = psum_s.tile([P, 2, P], F32, tag="s")
+        for m in range(2):
+            nc.tensor.transpose(
+                triT_ps[:, m, :], tri[:, m].rearrange("p t x -> p (t x)"), ident_f32[:]
+            )
+        triT = keep.tile([P, 2, P], F32)
+        nc.vector.tensor_copy(out=triT[:], in_=triT_ps[:])
+
+        for i in range(-1, N_PAIRS + 3):
+            if 0 <= i - 1 < N_PAIRS:
+                transpose_e(i - 1)
+            if i + 1 < N_PAIRS:
+                scores(i + 1, 0)
+                scores(i + 1, 1)
+            if 0 <= i < N_PAIRS:
+                exponentials(i, 0)
+                exponentials(i, 1)
+            if 0 <= i - 3 < N_PAIRS and (i - 3) % 2 == 1:
+                finish((i - 3) // 2)
+            if 0 <= i - 2 < N_PAIRS:
+                weighted_sum(i - 2)
+            if 0 <= i - 1 < N_PAIRS:
+                regroup_e(i - 1)
+            if 0 <= i < N_PAIRS:
+                regroup_v(i)
+            if i + 1 < N_PAIRS:
+                row_max(i + 1, 0)
+            if 0 <= i < N_PAIRS:
+                quantise_v(i)
+            if i + 1 < N_PAIRS:
+                row_max(i + 1, 1)
+            if i + STEPS_AHEAD < 2 * HEADS * CHUNKS:
+                transpose_step(i + STEPS_AHEAD)

@@ -112,7 +112,7 @@ def tile_sparseattention_kernel(tc, q, k, v, out):
                     in_=t_ps[:].rearrange("p t (b x) -> p t b x", x=BLOCK_X),
                 )
             else:
-                nc.scalar.copy(
+                nc.vector.tensor_copy(
                     out=qT[:, h, a * SPAN : (a + 1) * SPAN],
                     in_=t_ps[:].rearrange("p t i -> p (t i)"),
                 )
@@ -123,7 +123,10 @@ def tile_sparseattention_kernel(tc, q, k, v, out):
 
         def regroup_v(n):
             v_grouped = work.tile([P, DIM, PACK], BF16, align_bytes=64)
-            nc.vector.tensor_copy(out=v_grouped[:], in_=v_raw[:, n].rearrange("p t d -> p d t"))
+            nc.gpsimd.tensor_scalar(
+                out=v_grouped[:], in0=v_raw[:, n].rearrange("p t d -> p d t"),
+                scalar1=1.0, scalar2=0.0, op0=ALU.mult, op1=ALU.add,
+            )
             live[("v", n)] = v_grouped
 
         def quantise_v(n):
@@ -157,14 +160,13 @@ def tile_sparseattention_kernel(tc, q, k, v, out):
 
         def row_max(n, j):
             n_blocks = len(key_blocks(2 * (n % PAIRS) + j))
-            neg_max = small.tile([P, 1], F32)
-            nc.vector.tensor_reduce(
-                out=neg_max[:],
-                in_=live[("s", n, j)][:, :n_blocks].rearrange("p g t x -> p (g t x)"),
-                axis=AXIS.X, op=ALU.max, negate=True,
-            )
+            products = work.tile([P, 3 * BLOCK], BF16)
             bias = small.tile([P, 1], F32)
-            nc.vector.tensor_scalar_mul(out=bias[:], in0=neg_max[:], scalar1=SCALE)
+            nc.vector.tensor_scalar(
+                out=products[:, : n_blocks * BLOCK],
+                in0=live[("s", n, j)][:, :n_blocks].rearrange("p g t x -> p (g t x)"),
+                scalar1=-SCALE, scalar2=None, op0=ALU.mult, op1=ALU.min, accum_out=bias[:],
+            )
             live[("bias", n, j)] = bias
 
         def exponentials(n, j):
@@ -275,9 +277,8 @@ def tile_sparseattention_kernel(tc, q, k, v, out):
                 weighted_sum(i - 2)
             if 0 <= i - 1 < N_PAIRS:
                 regroup_e(i - 1)
-            if 0 <= i < N_PAIRS:
-                regroup_v(i)
             if i + 1 < N_PAIRS:
+                regroup_v(i + 1)
                 row_max(i + 1, 0)
             if 0 <= i < N_PAIRS:
                 quantise_v(i)

@@ -24,6 +24,8 @@ TILES = SEQ // Q_TILE
 PAIRS = TILES // 2
 N_PAIRS = HEADS * PAIRS
 CHUNKS = SEQ // SPAN
+N_STEPS = 2 * HEADS * CHUNKS
+FIRST_STEPS = 2
 STEPS_AHEAD = 3
 BLOCK = 128
 BLOCK_X = BLOCK // PACK
@@ -96,16 +98,22 @@ def tile_sparseattention_kernel(tc, q, k, v, out):
 
         kT = keep.tile([P, HEADS, TILES, PACK, BLOCK_X], BF16)
         qT = keep.tile([P, HEADS, SEQ], BF16)
+        live = {}
 
         def transpose_step(n):
             h, a = n // (2 * CHUNKS), (n // 2) % CHUNKS
             raw = k_raw if n % 2 == 0 else q_raw
-            if n < STEPS_AHEAD - 1:
+            if n < FIRST_STEPS:
                 t_ps = psum_2.tile([P, PACK, P], BF16, tag="eT")
             else:
                 t_ps = psum_1.tile([P, PACK, P], BF16, tag="tp")
             for t in range(PACK):
                 nc.tensor.transpose(t_ps[:, t, :], raw[:, h, a, t, :], ident[:])
+            live[("step", n)] = t_ps
+
+        def keep_step(n):
+            h, a = n // (2 * CHUNKS), (n // 2) % CHUNKS
+            t_ps = live[("step", n)]
             if n % 2 == 0:
                 nc.vector.tensor_copy(
                     out=kT[:, h, PACK * a : PACK * (a + 1)].rearrange("p b t x -> p t b x"),
@@ -119,7 +127,6 @@ def tile_sparseattention_kernel(tc, q, k, v, out):
 
         v_codes = keep.tile([P, N_PAIRS, DIM], U32, align_bytes=64)
         v_scales = keep.tile([P, N_PAIRS, DIM], U8, align_bytes=64)
-        live = {}
 
         def regroup_v(n):
             v_grouped = work.tile([P, DIM, PACK], BF16, align_bytes=64)
@@ -199,9 +206,11 @@ def tile_sparseattention_kernel(tc, q, k, v, out):
 
         def regroup_e(n):
             e_grouped = work.tile([P, 2, Q_TILE, PACK], BF16, align_bytes=64)
-            nc.scalar.copy(
-                out=e_grouped[:], in_=live[("eT", n)][:].rearrange("p j t i -> p j i t")
-            )
+            permuted = live[("eT", n)][:].rearrange("p j t i -> p j i t")
+            if n < N_PAIRS - 2:
+                nc.scalar.copy(out=e_grouped[:], in_=permuted)
+            else:
+                nc.vector.tensor_copy(out=e_grouped[:], in_=permuted)
             live[("eg", n)] = e_grouped
 
         def weighted_sum(n):
@@ -227,9 +236,13 @@ def tile_sparseattention_kernel(tc, q, k, v, out):
                     stop=True,
                 )
 
-        def finish(group):
+        def invert_sums(group):
             r_sums = small.tile([P, GROUP], F32)
             nc.vector.reciprocal(out=r_sums[:], in_=live[("sums", group)][:])
+            live[("1/sums", group)] = r_sums
+
+        def finish(group):
+            r_sums = live[("1/sums", group)]
             o_sb = work.tile([P, GROUP, DIM], F32)
             nc.vector.tensor_tensor(
                 out=o_sb[:], in0=live[("o", group)][:],
@@ -241,8 +254,10 @@ def tile_sparseattention_kernel(tc, q, k, v, out):
                 in_=o_sb[:],
             )
 
-        for n in range(STEPS_AHEAD - 1):
+        for n in range(FIRST_STEPS):
             transpose_step(n)
+            keep_step(n)
+        transpose_step(FIRST_STEPS)
 
         tri = keep.tile([P, 2, PACK, BLOCK_X], F32)
         nc.gpsimd.memset(tri[:], 0.0)
@@ -263,6 +278,8 @@ def tile_sparseattention_kernel(tc, q, k, v, out):
         nc.vector.tensor_copy(out=triT[:], in_=triT_ps[:])
 
         for i in range(-1, N_PAIRS + 3):
+            if i + STEPS_AHEAD < N_STEPS:
+                keep_step(i + STEPS_AHEAD)
             if 0 <= i - 1 < N_PAIRS:
                 transpose_e(i - 1)
             if i + 1 < N_PAIRS:
@@ -284,5 +301,7 @@ def tile_sparseattention_kernel(tc, q, k, v, out):
                 quantise_v(i)
             if i + 1 < N_PAIRS:
                 row_max(i + 1, 1)
-            if i + STEPS_AHEAD < 2 * HEADS * CHUNKS:
-                transpose_step(i + STEPS_AHEAD)
+            if 0 <= i - 2 < N_PAIRS and (i - 2) % 2 == 1:
+                invert_sums((i - 2) // 2)
+            if i + STEPS_AHEAD + 1 < N_STEPS:
+                transpose_step(i + STEPS_AHEAD + 1)

@@ -119,6 +119,11 @@ def tile_sparseattention_kernel(tc, q, k, v, out):
                     out=kT[:, h, PACK * a : PACK * (a + 1)].rearrange("p b t x -> p t b x"),
                     in_=t_ps[:].rearrange("p t (b x) -> p t b x", x=BLOCK_X),
                 )
+            elif n < FIRST_STEPS:
+                nc.scalar.copy(
+                    out=qT[:, h, a * SPAN : (a + 1) * SPAN],
+                    in_=t_ps[:].rearrange("p t i -> p (t i)"),
+                )
             else:
                 nc.vector.tensor_copy(
                     out=qT[:, h, a * SPAN : (a + 1) * SPAN],
@@ -127,20 +132,19 @@ def tile_sparseattention_kernel(tc, q, k, v, out):
 
         v_codes = keep.tile([P, N_PAIRS, DIM], U32, align_bytes=64)
         v_scales = keep.tile([P, N_PAIRS, DIM], U8, align_bytes=64)
+        v_grouped = keep.tile([P, DIM, PACK], BF16, align_bytes=64)
 
         def regroup_v(n):
-            v_grouped = work.tile([P, DIM, PACK], BF16, align_bytes=64)
             nc.gpsimd.tensor_scalar(
                 out=v_grouped[:], in0=v_raw[:, n].rearrange("p t d -> p d t"),
                 scalar1=1.0, scalar2=0.0, op0=ALU.mult, op1=ALU.add,
             )
-            live[("v", n)] = v_grouped
 
         def quantise_v(n):
             nc.vector.quantize_mx(
                 out=v_codes[:, n, :].bitcast(FP8X4),
                 scales=v_scales[:, n, :],
-                in_=live[("v", n)][:].rearrange("p d t -> p (d t)"),
+                in_=v_grouped[:].rearrange("p d t -> p (d t)"),
             )
 
         def scores(n, j):
@@ -183,17 +187,16 @@ def tile_sparseattention_kernel(tc, q, k, v, out):
             case = (x_lo, len(blocks))
             e_tile = e_tiles[(case, e_uses[case] % E_BUFS)]
             e_uses[case] += 1
-            if n % 2 == 0 and j == 0:
-                e_sums = small.tile([P, GROUP], F32)
-                live[("sums", n // 2)] = e_sums
-            g = 2 * (n % 2) + j
+            if j == 0:
+                e_sums = small.tile([P, 2], F32)
+                live[("sums", n)] = e_sums
             nc.scalar.activation(
                 out=e_tile[:, :, x_lo : x_lo + len(blocks) * BLOCK_X].rearrange(
                     "p t (g x) -> p g t x", x=BLOCK_X
                 ),
                 in_=live[("s", n, j)][:, : len(blocks)],
                 func=ACT.Exp, bias=live[("bias", n, j)][:], scale=SCALE,
-                accum_out=live[("sums", n // 2)][:, g : g + 1],
+                accum_out=live[("sums", n)][:, j : j + 1],
             )
             live[("e", n, j)] = e_tile
 
@@ -206,11 +209,9 @@ def tile_sparseattention_kernel(tc, q, k, v, out):
 
         def regroup_e(n):
             e_grouped = work.tile([P, 2, Q_TILE, PACK], BF16, align_bytes=64)
-            permuted = live[("eT", n)][:].rearrange("p j t i -> p j i t")
-            if n < N_PAIRS - 2:
-                nc.scalar.copy(out=e_grouped[:], in_=permuted)
-            else:
-                nc.vector.tensor_copy(out=e_grouped[:], in_=permuted)
+            nc.scalar.copy(
+                out=e_grouped[:], in_=live[("eT", n)][:].rearrange("p j t i -> p j i t")
+            )
             live[("eg", n)] = e_grouped
 
         def weighted_sum(n):
@@ -221,13 +222,12 @@ def tile_sparseattention_kernel(tc, q, k, v, out):
                 scales=e_scales[:],
                 in_=live[("eg", n)][:].rearrange("p j i t -> p (j i t)"),
             )
-            if n % 2 == 0:
-                o_ps = psum_1.tile([P, GROUP, DIM], F32, tag="o")
-                live[("o", n // 2)] = o_ps
+            o_ps = psum_1.tile([P, 2, DIM], F32, tag="o")
+            live[("o", n)] = o_ps
             for j in range(2):
                 cols = slice(j * Q_TILE, (j + 1) * Q_TILE)
                 nc.tensor.matmul_mx(
-                    out=live[("o", n // 2)][:, 2 * (n % 2) + j, :],
+                    out=o_ps[:, j, :],
                     lhsT=e_codes[:, cols].bitcast(FP8X4),
                     lhsT_scale=e_scales[:, cols],
                     rhs=v_codes[:, n, :].bitcast(FP8X4),
@@ -236,26 +236,26 @@ def tile_sparseattention_kernel(tc, q, k, v, out):
                     stop=True,
                 )
 
-        def invert_sums(group):
-            r_sums = small.tile([P, GROUP], F32)
-            nc.vector.reciprocal(out=r_sums[:], in_=live[("sums", group)][:])
-            live[("1/sums", group)] = r_sums
+        def invert_sums(n):
+            r_sums = small.tile([P, 2], F32)
+            nc.vector.reciprocal(out=r_sums[:], in_=live[("sums", n)][:])
+            live[("1/sums", n)] = r_sums
 
-        def finish(group):
-            r_sums = live[("1/sums", group)]
-            o_sb = work.tile([P, GROUP, DIM], F32)
+        def finish(n):
+            o_sb = work.tile([P, 2, DIM], F32)
             nc.vector.tensor_tensor(
-                out=o_sb[:], in0=live[("o", group)][:],
-                in1=r_sums[:].unsqueeze(2).to_broadcast([P, GROUP, DIM]), op=ALU.mult,
+                out=o_sb[:], in0=live[("o", n)][:],
+                in1=live[("1/sums", n)][:].unsqueeze(2).to_broadcast([P, 2, DIM]), op=ALU.mult,
             )
-            row0 = group * GROUP * Q_TILE
+            row0 = n * 2 * Q_TILE
             nc.sync.dma_start(
-                out=out_rows[row0 : row0 + GROUP * Q_TILE, :].rearrange("(g p) d -> p g d", p=P),
+                out=out_rows[row0 : row0 + 2 * Q_TILE, :].rearrange("(j p) d -> p j d", p=P),
                 in_=o_sb[:],
             )
 
         for n in range(FIRST_STEPS):
             transpose_step(n)
+        for n in range(FIRST_STEPS):
             keep_step(n)
         transpose_step(FIRST_STEPS)
 
@@ -288,20 +288,20 @@ def tile_sparseattention_kernel(tc, q, k, v, out):
             if 0 <= i < N_PAIRS:
                 exponentials(i, 0)
                 exponentials(i, 1)
-            if 0 <= i - 3 < N_PAIRS and (i - 3) % 2 == 1:
-                finish((i - 3) // 2)
+            if 0 <= i - 3 < N_PAIRS:
+                finish(i - 3)
             if 0 <= i - 2 < N_PAIRS:
                 weighted_sum(i - 2)
             if 0 <= i - 1 < N_PAIRS:
                 regroup_e(i - 1)
             if i + 1 < N_PAIRS:
-                regroup_v(i + 1)
                 row_max(i + 1, 0)
             if 0 <= i < N_PAIRS:
                 quantise_v(i)
             if i + 1 < N_PAIRS:
+                regroup_v(i + 1)
                 row_max(i + 1, 1)
-            if 0 <= i - 2 < N_PAIRS and (i - 2) % 2 == 1:
-                invert_sums((i - 2) // 2)
+            if 0 <= i - 2 < N_PAIRS:
+                invert_sums(i - 2)
             if i + STEPS_AHEAD + 1 < N_STEPS:
                 transpose_step(i + STEPS_AHEAD + 1)

@@ -132,19 +132,20 @@ def tile_sparseattention_kernel(tc, q, k, v, out):
 
         v_codes = keep.tile([P, N_PAIRS, DIM], U32, align_bytes=64)
         v_scales = keep.tile([P, N_PAIRS, DIM], U8, align_bytes=64)
-        v_grouped = keep.tile([P, DIM, PACK], BF16, align_bytes=64)
 
         def regroup_v(n):
+            v_grouped = work.tile([P, DIM, PACK], BF16, align_bytes=64)
             nc.gpsimd.tensor_scalar(
                 out=v_grouped[:], in0=v_raw[:, n].rearrange("p t d -> p d t"),
                 scalar1=1.0, scalar2=0.0, op0=ALU.mult, op1=ALU.add,
             )
+            live[("v", n)] = v_grouped
 
         def quantise_v(n):
             nc.vector.quantize_mx(
                 out=v_codes[:, n, :].bitcast(FP8X4),
                 scales=v_scales[:, n, :],
-                in_=v_grouped[:].rearrange("p d t -> p (d t)"),
+                in_=live[("v", n)][:].rearrange("p d t -> p (d t)"),
             )
 
         def scores(n, j):
@@ -295,11 +296,11 @@ def tile_sparseattention_kernel(tc, q, k, v, out):
             if 0 <= i - 1 < N_PAIRS:
                 regroup_e(i - 1)
             if i + 1 < N_PAIRS:
+                regroup_v(i + 1)
                 row_max(i + 1, 0)
             if 0 <= i < N_PAIRS:
                 quantise_v(i)
             if i + 1 < N_PAIRS:
-                regroup_v(i + 1)
                 row_max(i + 1, 1)
             if 0 <= i - 2 < N_PAIRS:
                 invert_sums(i - 2)

@@ -66,15 +66,10 @@ def tile_sparseattention_kernel(tc, q, k, v, out):
         for n in range(N_PAIRS):
             h, a = n // (2 * CHUNKS), (n // 2) % CHUNKS
             rows = slice(h * SEQ + a * SPAN, h * SEQ + (a + 1) * SPAN)
-            if n % 2 == 0:
-                nc.sync.dma_start(
-                    out=k_raw[:, h, a].rearrange("p t d -> p (t d)"),
-                    in_=k_rows[rows, :].rearrange("(p t) d -> p (t d)", t=PACK),
-                )
-            else:
-                nc.sync.dma_start(
-                    out=q_raw[:, h, a], in_=q_rows[rows, :].rearrange("(n p) d -> p n d", p=P)
-                )
+            raw, dram = (k_raw, k_rows) if n % 2 == 0 else (q_raw, q_rows)
+            nc.sync.dma_start(
+                out=raw[:, h, a], in_=dram[rows, :].rearrange("(b p) d -> p b d", p=P)
+            )
             c = (n // PAIRS) * SEQ + span_start(n % PAIRS)
             nc.sync.dma_start(
                 out=v_raw[:, n].rearrange("p t d -> p (t d)"),
@@ -86,6 +81,17 @@ def tile_sparseattention_kernel(tc, q, k, v, out):
         ident_f32 = keep.tile([P, P], F32)
         make_identity(nc, ident_f32[:])
 
+        triT = keep.tile([P, 2, P], F32)
+        nc.gpsimd.memset(triT[:], 0.0)
+        nc.gpsimd.affine_select(
+            out=triT[:, 0, :], in_=triT[:, 0, :], pattern=[[-1, P]],
+            compare_op=ALU.is_ge, fill=MASKED, base=0, channel_multiplier=1,
+        )
+        nc.gpsimd.affine_select(
+            out=triT[:, 1, :], in_=triT[:, 1, :], pattern=[[1, P]],
+            compare_op=ALU.is_ge, fill=MASKED, base=-1, channel_multiplier=-1,
+        )
+
         E_BUFS = 2
         e_tiles = {}
         e_uses = {}
@@ -96,7 +102,7 @@ def tile_sparseattention_kernel(tc, q, k, v, out):
                 nc.vector.memset(e_tile[:], 0.0)
                 e_tiles[(case, b)] = e_tile
 
-        kT = keep.tile([P, HEADS, TILES, PACK, BLOCK_X], BF16)
+        kT = keep.tile([P, HEADS, SEQ], BF16)
         qT = keep.tile([P, HEADS, SEQ], BF16)
         live = {}
 
@@ -113,48 +119,38 @@ def tile_sparseattention_kernel(tc, q, k, v, out):
 
         def keep_step(n):
             h, a = n // (2 * CHUNKS), (n // 2) % CHUNKS
-            t_ps = live[("step", n)]
-            if n % 2 == 0:
-                nc.vector.tensor_copy(
-                    out=kT[:, h, PACK * a : PACK * (a + 1)].rearrange("p b t x -> p t b x"),
-                    in_=t_ps[:].rearrange("p t (b x) -> p t b x", x=BLOCK_X),
-                )
-            elif n < FIRST_STEPS:
-                nc.scalar.copy(
-                    out=qT[:, h, a * SPAN : (a + 1) * SPAN],
-                    in_=t_ps[:].rearrange("p t i -> p (t i)"),
-                )
+            transposed = kT if n % 2 == 0 else qT
+            place = transposed[:, h, a * SPAN : (a + 1) * SPAN]
+            rows = live[("step", n)][:].rearrange("p b i -> p (b i)")
+            if n == 1:
+                nc.scalar.copy(out=place, in_=rows)
             else:
-                nc.vector.tensor_copy(
-                    out=qT[:, h, a * SPAN : (a + 1) * SPAN],
-                    in_=t_ps[:].rearrange("p t i -> p (t i)"),
-                )
+                nc.vector.tensor_copy(out=place, in_=rows)
 
         v_codes = keep.tile([P, N_PAIRS, DIM], U32, align_bytes=64)
         v_scales = keep.tile([P, N_PAIRS, DIM], U8, align_bytes=64)
+        v_grouped = keep.tile([P, DIM, PACK], BF16, align_bytes=64)
 
         def regroup_v(n):
-            v_grouped = work.tile([P, DIM, PACK], BF16, align_bytes=64)
             nc.gpsimd.tensor_scalar(
                 out=v_grouped[:], in0=v_raw[:, n].rearrange("p t d -> p d t"),
                 scalar1=1.0, scalar2=0.0, op0=ALU.mult, op1=ALU.add,
             )
-            live[("v", n)] = v_grouped
 
         def quantise_v(n):
             nc.vector.quantize_mx(
                 out=v_codes[:, n, :].bitcast(FP8X4),
                 scales=v_scales[:, n, :],
-                in_=live[("v", n)][:].rearrange("p d t -> p (d t)"),
+                in_=v_grouped[:].rearrange("p d t -> p (d t)"),
             )
 
         def scores(n, j):
             h, t_idx = n // PAIRS, 2 * (n % PAIRS) + j
-            s_ps = psum_s.tile([P, 3, PACK, BLOCK_X], F32, tag="s")
+            s_ps = psum_s.tile([P, 3, BLOCK], F32, tag="s")
             for g, b in enumerate(key_blocks(t_idx)):
                 if b != t_idx:
                     nc.tensor.matmul(
-                        s_ps[:, g].rearrange("p t x -> p (t x)"),
+                        s_ps[:, g, :],
                         lhsT=triT[:, 0 if b < t_idx else 1, :],
                         rhs=ident_f32[:],
                         is_transpose=True,
@@ -162,9 +158,9 @@ def tile_sparseattention_kernel(tc, q, k, v, out):
                         stop=False,
                     )
                 nc.tensor.matmul(
-                    s_ps[:, g].rearrange("p t x -> p (t x)"),
+                    s_ps[:, g, :],
                     lhsT=qT[:, h, t_idx * Q_TILE : (t_idx + 1) * Q_TILE],
-                    rhs=kT[:, h, b].rearrange("p t x -> p (t x)"),
+                    rhs=kT[:, h, b * BLOCK : (b + 1) * BLOCK],
                     start=(b == t_idx),
                     stop=True,
                 )
@@ -176,7 +172,7 @@ def tile_sparseattention_kernel(tc, q, k, v, out):
             bias = small.tile([P, 1], F32)
             nc.vector.tensor_scalar(
                 out=products[:, : n_blocks * BLOCK],
-                in0=live[("s", n, j)][:, :n_blocks].rearrange("p g t x -> p (g t x)"),
+                in0=live[("s", n, j)][:, :n_blocks].rearrange("p g c -> p (g c)"),
                 scalar1=-SCALE, scalar2=None, op0=ALU.mult, op1=ALU.min, accum_out=bias[:],
             )
             live[("bias", n, j)] = bias
@@ -195,7 +191,7 @@ def tile_sparseattention_kernel(tc, q, k, v, out):
                 out=e_tile[:, :, x_lo : x_lo + len(blocks) * BLOCK_X].rearrange(
                     "p t (g x) -> p g t x", x=BLOCK_X
                 ),
-                in_=live[("s", n, j)][:, : len(blocks)],
+                in_=live[("s", n, j)][:, : len(blocks)].rearrange("p g (x t) -> p g t x", t=PACK),
                 func=ACT.Exp, bias=live[("bias", n, j)][:], scale=SCALE,
                 accum_out=live[("sums", n)][:, j : j + 1],
             )
@@ -260,24 +256,6 @@ def tile_sparseattention_kernel(tc, q, k, v, out):
             keep_step(n)
         transpose_step(FIRST_STEPS)
 
-        tri = keep.tile([P, 2, PACK, BLOCK_X], F32)
-        nc.gpsimd.memset(tri[:], 0.0)
-        nc.gpsimd.affine_select(
-            out=tri[:, 0], in_=tri[:, 0], pattern=[[1, PACK], [PACK, BLOCK_X]],
-            compare_op=ALU.is_ge, fill=MASKED, base=0, channel_multiplier=-1,
-        )
-        nc.gpsimd.affine_select(
-            out=tri[:, 1], in_=tri[:, 1], pattern=[[-1, PACK], [-PACK, BLOCK_X]],
-            compare_op=ALU.is_ge, fill=MASKED, base=-1, channel_multiplier=1,
-        )
-        triT_ps = psum_s.tile([P, 2, P], F32, tag="s")
-        for m in range(2):
-            nc.tensor.transpose(
-                triT_ps[:, m, :], tri[:, m].rearrange("p t x -> p (t x)"), ident_f32[:]
-            )
-        triT = keep.tile([P, 2, P], F32)
-        nc.vector.tensor_copy(out=triT[:], in_=triT_ps[:])
-
         for i in range(-1, N_PAIRS + 3):
             if i + STEPS_AHEAD < N_STEPS:
                 keep_step(i + STEPS_AHEAD)
@@ -296,11 +274,11 @@ def tile_sparseattention_kernel(tc, q, k, v, out):
             if 0 <= i - 1 < N_PAIRS:
                 regroup_e(i - 1)
             if i + 1 < N_PAIRS:
-                regroup_v(i + 1)
                 row_max(i + 1, 0)
             if 0 <= i < N_PAIRS:
                 quantise_v(i)
             if i + 1 < N_PAIRS:
+                regroup_v(i + 1)
                 row_max(i + 1, 1)
             if 0 <= i - 2 < N_PAIRS:
                 invert_sums(i - 2)

@@ -98,7 +98,7 @@ def tile_sparseattention_kernel(tc, q, k, v, out):
         for case in ((0, 2), (0, 3), (BLOCK_X, 3), (2 * BLOCK_X, 2)):
             e_uses[case] = 0
             for b in range(E_BUFS):
-                e_tile = keep.tile([P, PACK, P], BF16, name="e%d_%d_%d" % (case[0], case[1], b))
+                e_tile = keep.tile([P, 2, P, 2], BF16, name="e%d_%d_%d" % (case[0], case[1], b))
                 nc.vector.memset(e_tile[:], 0.0)
                 e_tiles[(case, b)] = e_tile
 
@@ -120,12 +120,12 @@ def tile_sparseattention_kernel(tc, q, k, v, out):
         def keep_step(n):
             h, a = n // (2 * CHUNKS), (n // 2) % CHUNKS
             transposed = kT if n % 2 == 0 else qT
-            place = transposed[:, h, a * SPAN : (a + 1) * SPAN]
-            rows = live[("step", n)][:].rearrange("p b i -> p (b i)")
-            if n == 1:
-                nc.scalar.copy(out=place, in_=rows)
-            else:
+            place = transposed[:, h, a * SPAN : (a + 1) * SPAN].bitcast(F32)
+            rows = live[("step", n)][:].rearrange("p b i -> p (b i)").bitcast(F32)
+            if n == 0:
                 nc.vector.tensor_copy(out=place, in_=rows)
+            else:
+                nc.scalar.copy(out=place, in_=rows)
 
         v_codes = keep.tile([P, N_PAIRS, DIM], U32, align_bytes=64)
         v_scales = keep.tile([P, N_PAIRS, DIM], U8, align_bytes=64)
@@ -188,26 +188,31 @@ def tile_sparseattention_kernel(tc, q, k, v, out):
                 e_sums = small.tile([P, 2], F32)
                 live[("sums", n)] = e_sums
             nc.scalar.activation(
-                out=e_tile[:, :, x_lo : x_lo + len(blocks) * BLOCK_X].rearrange(
-                    "p t (g x) -> p g t x", x=BLOCK_X
-                ),
-                in_=live[("s", n, j)][:, : len(blocks)].rearrange("p g (x t) -> p g t x", t=PACK),
+                out=e_tile[:, :, x_lo : x_lo + len(blocks) * BLOCK_X, :],
+                in_=live[("s", n, j)][:, : len(blocks)]
+                .rearrange("p g c -> p (g c)")
+                .rearrange("p (x u i) -> p u x i", u=2, i=2),
                 func=ACT.Exp, bias=live[("bias", n, j)][:], scale=SCALE,
                 accum_out=live[("sums", n)][:, j : j + 1],
             )
             live[("e", n, j)] = e_tile
 
         def transpose_e(n):
-            eT_ps = psum_2.tile([P, 2, PACK, Q_TILE], BF16, tag="eT")
+            eT_ps = psum_2.tile([P, 2, 2, Q_TILE], F32, tag="eT")
             for j in range(2):
-                for t in range(PACK):
-                    nc.tensor.transpose(eT_ps[:, j, t, :], live[("e", n, j)][:, t, :], ident[:])
+                for u in range(2):
+                    words = live[("e", n, j)][:, u].rearrange("p x i -> p (x i)").bitcast(F32)
+                    nc.tensor.transpose(eT_ps[:, j, u, :], words, ident_f32[:])
             live[("eT", n)] = eT_ps
 
         def regroup_e(n):
             e_grouped = work.tile([P, 2, Q_TILE, PACK], BF16, align_bytes=64)
             nc.scalar.copy(
-                out=e_grouped[:], in_=live[("eT", n)][:].rearrange("p j t i -> p j i t")
+                out=e_grouped[:]
+                .rearrange("p j i t -> p (j i t)")
+                .bitcast(F32)
+                .rearrange("p (j i u) -> p j i u", j=2, u=2),
+                in_=live[("eT", n)][:].rearrange("p j u i -> p j i u"),
             )
             live[("eg", n)] = e_grouped
 
@@ -257,8 +262,6 @@ def tile_sparseattention_kernel(tc, q, k, v, out):
         transpose_step(FIRST_STEPS)
 
         for i in range(-1, N_PAIRS + 3):
-            if i + STEPS_AHEAD < N_STEPS:
-                keep_step(i + STEPS_AHEAD)
             if 0 <= i - 1 < N_PAIRS:
                 transpose_e(i - 1)
             if i + 1 < N_PAIRS:
@@ -267,6 +270,8 @@ def tile_sparseattention_kernel(tc, q, k, v, out):
             if 0 <= i < N_PAIRS:
                 exponentials(i, 0)
                 exponentials(i, 1)
+            if i + STEPS_AHEAD < N_STEPS:
+                keep_step(i + STEPS_AHEAD)
             if 0 <= i - 3 < N_PAIRS:
                 finish(i - 3)
             if 0 <= i - 2 < N_PAIRS:

@@ -26,7 +26,7 @@ N_PAIRS = HEADS * PAIRS
 CHUNKS = SEQ // SPAN
 N_STEPS = 2 * HEADS * CHUNKS
 FIRST_STEPS = 2
-STEPS_AHEAD = 3
+STEPS_AHEAD = 4
 BLOCK = 128
 BLOCK_X = BLOCK // PACK
 GROUP = 4
@@ -99,7 +99,10 @@ def tile_sparseattention_kernel(tc, q, k, v, out):
             e_uses[case] = 0
             for b in range(E_BUFS):
                 e_tile = keep.tile([P, 2, P, 2], BF16, name="e%d_%d_%d" % (case[0], case[1], b))
-                nc.vector.memset(e_tile[:], 0.0)
+                seen = (case[0], case[0] + case[1] * BLOCK_X)
+                for lo, hi in ((0, seen[0]), (seen[1], P)):
+                    if lo < hi:
+                        nc.vector.memset(e_tile[:, :, lo:hi, :], 0.0)
                 e_tiles[(case, b)] = e_tile
 
         kT = keep.tile([P, HEADS, SEQ], BF16)
@@ -216,7 +219,7 @@ def tile_sparseattention_kernel(tc, q, k, v, out):
             )
             live[("eg", n)] = e_grouped
 
-        def weighted_sum(n):
+        def quantise_e(n):
             e_codes = work.tile([P, 2 * Q_TILE], U32, align_bytes=64)
             e_scales = work.tile([P, 2 * Q_TILE], U8, align_bytes=64)
             nc.vector.quantize_mx(
@@ -224,6 +227,10 @@ def tile_sparseattention_kernel(tc, q, k, v, out):
                 scales=e_scales[:],
                 in_=live[("eg", n)][:].rearrange("p j i t -> p (j i t)"),
             )
+            live[("ec", n)] = (e_codes, e_scales)
+
+        def weighted_sum(n):
+            e_codes, e_scales = live[("ec", n)]
             o_ps = psum_1.tile([P, 2, DIM], F32, tag="o")
             live[("o", n)] = o_ps
             for j in range(2):
@@ -261,31 +268,35 @@ def tile_sparseattention_kernel(tc, q, k, v, out):
             keep_step(n)
         transpose_step(FIRST_STEPS)
 
-        for i in range(-1, N_PAIRS + 3):
+        for i in range(-2, N_PAIRS + 2):
+            before, now, after, later = [0 <= i + d < N_PAIRS for d in (-2, 0, 1, 2)]
+            if before:
+                quantise_e(i - 2)
+            if after:
+                row_max(i + 1, 0)
+                row_max(i + 1, 1)
             if 0 <= i - 1 < N_PAIRS:
                 transpose_e(i - 1)
-            if i + 1 < N_PAIRS:
-                scores(i + 1, 0)
-                scores(i + 1, 1)
-            if 0 <= i < N_PAIRS:
+            if now:
                 exponentials(i, 0)
+            if later:
+                scores(i + 2, 0)
+            if before:
+                weighted_sum(i - 2)
+            if now:
                 exponentials(i, 1)
+            if later:
+                scores(i + 2, 1)
             if i + STEPS_AHEAD < N_STEPS:
                 keep_step(i + STEPS_AHEAD)
-            if 0 <= i - 3 < N_PAIRS:
-                finish(i - 3)
-            if 0 <= i - 2 < N_PAIRS:
-                weighted_sum(i - 2)
             if 0 <= i - 1 < N_PAIRS:
                 regroup_e(i - 1)
-            if i + 1 < N_PAIRS:
-                row_max(i + 1, 0)
-            if 0 <= i < N_PAIRS:
+            if now:
                 quantise_v(i)
-            if i + 1 < N_PAIRS:
+            if after:
                 regroup_v(i + 1)
-                row_max(i + 1, 1)
-            if 0 <= i - 2 < N_PAIRS:
+            if before:
                 invert_sums(i - 2)
+                finish(i - 2)
             if i + STEPS_AHEAD + 1 < N_STEPS:
                 transpose_step(i + STEPS_AHEAD + 1)

@@ -29,7 +29,7 @@ FIRST_STEPS = 2
 STEPS_AHEAD = 4
 BLOCK = 128
 BLOCK_X = BLOCK // PACK
-GROUP = 4
+EDGE_TILES = 2
 SCALE = 1.0 / DIM**0.5
 MASKED = -1.0e30
 
@@ -92,6 +92,17 @@ def tile_sparseattention_kernel(tc, q, k, v, out):
             compare_op=ALU.is_ge, fill=MASKED, base=-1, channel_multiplier=-1,
         )
 
+        tri = keep.tile([P, 2, P], BF16)
+        nc.gpsimd.memset(tri[:], 0.0)
+        nc.gpsimd.affine_select(
+            out=tri[:, 0, :], in_=tri[:, 0, :], pattern=[[1, P]],
+            compare_op=ALU.is_ge, fill=MASKED, base=0, channel_multiplier=-1,
+        )
+        nc.gpsimd.affine_select(
+            out=tri[:, 1, :], in_=tri[:, 1, :], pattern=[[-1, P]],
+            compare_op=ALU.is_ge, fill=MASKED, base=-1, channel_multiplier=1,
+        )
+
         E_BUFS = 2
         e_tiles = {}
         e_uses = {}
@@ -150,6 +161,21 @@ def tile_sparseattention_kernel(tc, q, k, v, out):
         def scores(n, j):
             h, t_idx = n // PAIRS, 2 * (n % PAIRS) + j
             s_ps = psum_s.tile([P, 3, BLOCK], F32, tag="s")
+            live[("s", n, j)] = s_ps
+            queries = qT[:, h, t_idx * Q_TILE : (t_idx + 1) * Q_TILE]
+            if EDGE_TILES <= t_idx < TILES - EDGE_TILES:
+                keys = kT[:, h, :].rearrange("p (b c) -> p b c", c=BLOCK)
+                nc.tensor.matmul(
+                    s_ps[:, 0:3:2, :], lhsT=ident[:], rhs=tri[:], start=True, stop=False
+                )
+                nc.tensor.matmul(
+                    s_ps[:, 0:3:2, :], lhsT=queries, rhs=keys[:, t_idx - 1 : t_idx + 2 : 2, :],
+                    start=False, stop=True,
+                )
+                nc.tensor.matmul(
+                    s_ps[:, 1, :], lhsT=queries, rhs=keys[:, t_idx, :], start=True, stop=True
+                )
+                return
             for g, b in enumerate(key_blocks(t_idx)):
                 if b != t_idx:
                     nc.tensor.matmul(
@@ -162,12 +188,11 @@ def tile_sparseattention_kernel(tc, q, k, v, out):
                     )
                 nc.tensor.matmul(
                     s_ps[:, g, :],
-                    lhsT=qT[:, h, t_idx * Q_TILE : (t_idx + 1) * Q_TILE],
+                    lhsT=queries,
                     rhs=kT[:, h, b * BLOCK : (b + 1) * BLOCK],
                     start=(b == t_idx),
                     stop=True,
                 )
-            live[("s", n, j)] = s_ps
 
         def row_max(n, j):
             n_blocks = len(key_blocks(2 * (n % PAIRS) + j))

@@ -297,7 +297,10 @@ def tile_sparseattention_kernel(tc, q, k, v, out):
             before, now, after, later = [0 <= i + d < N_PAIRS for d in (-2, 0, 1, 2)]
             if before:
                 quantise_e(i - 2)
+            if now:
+                quantise_v(i)
             if after:
+                regroup_v(i + 1)
                 row_max(i + 1, 0)
                 row_max(i + 1, 1)
             if 0 <= i - 1 < N_PAIRS:
@@ -316,10 +319,6 @@ def tile_sparseattention_kernel(tc, q, k, v, out):
                 keep_step(i + STEPS_AHEAD)
             if 0 <= i - 1 < N_PAIRS:
                 regroup_e(i - 1)
-            if now:
-                quantise_v(i)
-            if after:
-                regroup_v(i + 1)
             if before:
                 invert_sums(i - 2)
                 finish(i - 2)

@@ -17,16 +17,12 @@ PACK = 4
 HEADS = 2
 SEQ = 2048
 DIM = 128
-HALF = 128
 SPAN = P * PACK
 Q_TILE = P
 TILES = SEQ // Q_TILE
-PAIRS = TILES // 2
-N_PAIRS = HEADS * PAIRS
-CHUNKS = SEQ // SPAN
-N_STEPS = 2 * HEADS * CHUNKS
-FIRST_STEPS = 2
-STEPS_AHEAD = 4
+BLOCKS = HEADS * TILES
+STEP = 2
+N_STEPS = BLOCKS // STEP
 BLOCK = 128
 BLOCK_X = BLOCK // PACK
 EDGE_TILES = 2
@@ -35,13 +31,22 @@ MASKED = -1.0e30
 
 FLOPS = 2 * 2 * HEADS * SEQ * SPAN * DIM
 
+HEAD_STEPS = 2
+SPANS = (TILES - 2) // 2
+GROUPS = [[0]] + [[t, t + 1] for t in range(1, BLOCKS - 1, 2)] + [[BLOCKS - 1]]
+N_GROUPS = len(GROUPS)
 
-def span_start(pair):
-    return min(max(2 * Q_TILE * pair - HALF, 0), SEQ - SPAN)
+
+def span_of(t):
+    return SPANS * (t // TILES) + min(max((t % TILES - 1) // 2, 0), SPANS - 1)
 
 
-def key_blocks(t_idx):
-    return [b for b in (t_idx - 1, t_idx, t_idx + 1) if 0 <= b < TILES]
+def span_block(span):
+    return (span // SPANS) * TILES + 2 * (span % SPANS)
+
+
+def key_blocks(t):
+    return [b for b in (t - 1, t, t + 1) if 0 <= b < BLOCKS and b // TILES == t // TILES]
 
 
 def tile_sparseattention_kernel(tc, q, k, v, out):
@@ -60,21 +65,34 @@ def tile_sparseattention_kernel(tc, q, k, v, out):
         psum_1 = ctx.enter_context(tc.psum_pool(name="psum_1", bufs=1))
         ctx.enter_context(tc.manual_schedule())
 
-        k_raw = keep.tile([P, HEADS, CHUNKS, PACK, DIM], BF16)
-        q_raw = keep.tile([P, HEADS, CHUNKS, PACK, DIM], BF16)
-        v_raw = keep.tile([P, N_PAIRS, PACK, DIM], BF16)
-        for n in range(N_PAIRS):
-            h, a = n // (2 * CHUNKS), (n // 2) % CHUNKS
-            rows = slice(h * SEQ + a * SPAN, h * SEQ + (a + 1) * SPAN)
-            raw, dram = (k_raw, k_rows) if n % 2 == 0 else (q_raw, q_rows)
+        k_raw = keep.tile([P, BLOCKS, DIM], BF16)
+        q_raw = keep.tile([P, BLOCKS, DIM], BF16)
+        v_raw = keep.tile([P, HEADS * SPANS, PACK, DIM], BF16)
+
+        def load_steps(first, last):
+            blocks = slice(first * STEP, last * STEP)
+            rows = slice(first * STEP * BLOCK, last * STEP * BLOCK)
+            for raw, dram in ((k_raw, k_rows), (q_raw, q_rows)):
+                nc.sync.dma_start(
+                    out=raw[:, blocks, :], in_=dram[rows, :].rearrange("(b p) d -> p b d", p=P)
+                )
+
+        def load_span(span):
+            c = span_block(span) * BLOCK
             nc.sync.dma_start(
-                out=raw[:, h, a], in_=dram[rows, :].rearrange("(b p) d -> p b d", p=P)
-            )
-            c = (n // PAIRS) * SEQ + span_start(n % PAIRS)
-            nc.sync.dma_start(
-                out=v_raw[:, n].rearrange("p t d -> p (t d)"),
+                out=v_raw[:, span].rearrange("p t d -> p (t d)"),
                 in_=v_rows[c : c + SPAN, :].rearrange("(p t) d -> p (t d)", t=PACK),
             )
+
+        for first in range(HEAD_STEPS):
+            load_steps(first, first + 1)
+        loaded = 0
+        for first in range(HEAD_STEPS, N_STEPS + STEP, 2):
+            if first < N_STEPS:
+                load_steps(first, first + 2)
+            while loaded < HEADS * SPANS and loaded <= span_of(GROUPS[first - 1][-1]):
+                load_span(loaded)
+                loaded += 1
 
         ident = keep.tile([P, P], BF16)
         make_identity(nc, ident[:])
@@ -116,211 +134,259 @@ def tile_sparseattention_kernel(tc, q, k, v, out):
                         nc.vector.memset(e_tile[:, :, lo:hi, :], 0.0)
                 e_tiles[(case, b)] = e_tile
 
-        kT = keep.tile([P, HEADS, SEQ], BF16)
-        qT = keep.tile([P, HEADS, SEQ], BF16)
+        kqT = keep.tile([P, N_STEPS, 2 * STEP, BLOCK], BF16)
         live = {}
 
-        def transpose_step(n):
-            h, a = n // (2 * CHUNKS), (n // 2) % CHUNKS
-            raw = k_raw if n % 2 == 0 else q_raw
-            if n < FIRST_STEPS:
-                t_ps = psum_2.tile([P, PACK, P], BF16, tag="eT")
-            else:
-                t_ps = psum_1.tile([P, PACK, P], BF16, tag="tp")
-            for t in range(PACK):
-                nc.tensor.transpose(t_ps[:, t, :], raw[:, h, a, t, :], ident[:])
-            live[("step", n)] = t_ps
+        def transpose_step(s):
+            t_ps = psum_1.tile([P, 2 * STEP, P], BF16, tag="o" if s == 2 else "tp")
+            for b in range(STEP):
+                nc.tensor.transpose(t_ps[:, b, :], k_raw[:, s * STEP + b, :], ident[:])
+            for b in range(STEP):
+                nc.tensor.transpose(t_ps[:, STEP + b, :], q_raw[:, s * STEP + b, :], ident[:])
+            live[("step", s)] = t_ps
 
-        def keep_step(n):
-            h, a = n // (2 * CHUNKS), (n // 2) % CHUNKS
-            transposed = kT if n % 2 == 0 else qT
-            place = transposed[:, h, a * SPAN : (a + 1) * SPAN].bitcast(F32)
-            rows = live[("step", n)][:].rearrange("p b i -> p (b i)").bitcast(F32)
-            if n == 0:
-                nc.vector.tensor_copy(out=place, in_=rows)
-            else:
-                nc.scalar.copy(out=place, in_=rows)
+        def keep_step(s, copy):
+            copy(
+                out=kqT[:, s].rearrange("p b i -> p (b i)").bitcast(F32),
+                in_=live[("step", s)][:].rearrange("p b i -> p (b i)").bitcast(F32),
+            )
 
-        v_codes = keep.tile([P, N_PAIRS, DIM], U32, align_bytes=64)
-        v_scales = keep.tile([P, N_PAIRS, DIM], U8, align_bytes=64)
+        def first_step():
+            k_ps = psum_2.tile([P, STEP, P], BF16, tag="eT")
+            q_ps = psum_2.tile([P, STEP, P], BF16, tag="eT")
+            for t_ps, raw in ((k_ps, k_raw), (q_ps, q_raw)):
+                for b in range(STEP):
+                    nc.tensor.transpose(t_ps[:, b, :], raw[:, b, :], ident[:])
+            for t_ps, copy, lo in (
+                (k_ps, nc.vector.tensor_copy, 0),
+                (q_ps, nc.scalar.copy, STEP),
+            ):
+                copy(
+                    out=kqT[:, 0, lo : lo + STEP].rearrange("p b i -> p (b i)").bitcast(F32),
+                    in_=t_ps[:].rearrange("p b i -> p (b i)").bitcast(F32),
+                )
+
+        v_codes = keep.tile([P, HEADS * SPANS, DIM], U32, align_bytes=64)
+        v_scales = keep.tile([P, HEADS * SPANS, DIM], U8, align_bytes=64)
         v_grouped = keep.tile([P, DIM, PACK], BF16, align_bytes=64)
 
-        def regroup_v(n):
+        def regroup_v(span):
             nc.gpsimd.tensor_scalar(
-                out=v_grouped[:], in0=v_raw[:, n].rearrange("p t d -> p d t"),
+                out=v_grouped[:], in0=v_raw[:, span].rearrange("p t d -> p d t"),
                 scalar1=1.0, scalar2=0.0, op0=ALU.mult, op1=ALU.add,
             )
 
-        def quantise_v(n):
+        def quantise_v(span):
             nc.vector.quantize_mx(
-                out=v_codes[:, n, :].bitcast(FP8X4),
-                scales=v_scales[:, n, :],
+                out=v_codes[:, span, :].bitcast(FP8X4),
+                scales=v_scales[:, span, :],
                 in_=v_grouped[:].rearrange("p d t -> p (d t)"),
             )
 
-        def scores(n, j):
-            h, t_idx = n // PAIRS, 2 * (n % PAIRS) + j
+        def scores(t):
             s_ps = psum_s.tile([P, 3, BLOCK], F32, tag="s")
-            live[("s", n, j)] = s_ps
-            queries = qT[:, h, t_idx * Q_TILE : (t_idx + 1) * Q_TILE]
-            if EDGE_TILES <= t_idx < TILES - EDGE_TILES:
-                keys = kT[:, h, :].rearrange("p (b c) -> p b c", c=BLOCK)
+            live[("s", t)] = s_ps
+            queries = kqT[:, t // STEP, STEP + t % STEP, :]
+            if EDGE_TILES <= t % TILES < TILES - EDGE_TILES:
                 nc.tensor.matmul(
                     s_ps[:, 0:3:2, :], lhsT=ident[:], rhs=tri[:], start=True, stop=False
                 )
+                before = (t - 1) // STEP
                 nc.tensor.matmul(
-                    s_ps[:, 0:3:2, :], lhsT=queries, rhs=keys[:, t_idx - 1 : t_idx + 2 : 2, :],
-                    start=False, stop=True,
+                    s_ps[:, 0:3:2, :], lhsT=queries,
+                    rhs=kqT[:, before : before + 2, (t - 1) % STEP, :], start=False, stop=True,
                 )
                 nc.tensor.matmul(
-                    s_ps[:, 1, :], lhsT=queries, rhs=keys[:, t_idx, :], start=True, stop=True
+                    s_ps[:, 1, :], lhsT=queries, rhs=kqT[:, t // STEP, t % STEP, :],
+                    start=True, stop=True,
                 )
                 return
-            for g, b in enumerate(key_blocks(t_idx)):
-                if b != t_idx:
+            for g, b in enumerate(key_blocks(t)):
+                if b != t:
                     nc.tensor.matmul(
-                        s_ps[:, g, :],
-                        lhsT=triT[:, 0 if b < t_idx else 1, :],
-                        rhs=ident_f32[:],
-                        is_transpose=True,
-                        start=True,
-                        stop=False,
+                        s_ps[:, g, :], lhsT=triT[:, 0 if b < t else 1, :], rhs=ident_f32[:],
+                        is_transpose=True, start=True, stop=False,
                     )
                 nc.tensor.matmul(
-                    s_ps[:, g, :],
-                    lhsT=queries,
-                    rhs=kT[:, h, b * BLOCK : (b + 1) * BLOCK],
-                    start=(b == t_idx),
-                    stop=True,
+                    s_ps[:, g, :], lhsT=queries, rhs=kqT[:, b // STEP, b % STEP, :],
+                    start=(b == t), stop=True,
                 )
 
-        def row_max(n, j):
-            n_blocks = len(key_blocks(2 * (n % PAIRS) + j))
-            products = work.tile([P, 3 * BLOCK], BF16)
-            bias = small.tile([P, 1], F32)
-            nc.vector.tensor_scalar(
-                out=products[:, : n_blocks * BLOCK],
-                in0=live[("s", n, j)][:, :n_blocks].rearrange("p g c -> p (g c)"),
-                scalar1=-SCALE, scalar2=None, op0=ALU.mult, op1=ALU.min, accum_out=bias[:],
+        def row_max(g):
+            tiles = GROUPS[g]
+            least = small.tile([P, 2], F32)
+            bias = small.tile([P, 2], F32)
+            for j, t in enumerate(tiles):
+                nc.vector.tensor_reduce(
+                    out=least[:, j : j + 1],
+                    in_=live[("s", t)][:, : len(key_blocks(t))].rearrange("p g c -> p (g c)"),
+                    axis=AXIS.X, op=ALU.max, negate=True,
+                )
+            nc.gpsimd.tensor_scalar(
+                out=bias[:, : len(tiles)], in0=least[:, : len(tiles)],
+                scalar1=SCALE, scalar2=0.0, op0=ALU.mult, op1=ALU.add,
             )
-            live[("bias", n, j)] = bias
+            live[("bias", g)] = bias
 
-        def exponentials(n, j):
-            t_idx = 2 * (n % PAIRS) + j
-            blocks = key_blocks(t_idx)
-            x_lo = (BLOCK * blocks[0] - span_start(n % PAIRS)) // PACK
+        def exponentials(g, j):
+            t = GROUPS[g][j]
+            blocks = key_blocks(t)
+            x_lo = (blocks[0] - span_block(span_of(t))) * BLOCK_X
             case = (x_lo, len(blocks))
             e_tile = e_tiles[(case, e_uses[case] % E_BUFS)]
             e_uses[case] += 1
             if j == 0:
                 e_sums = small.tile([P, 2], F32)
-                live[("sums", n)] = e_sums
+                live[("sums", g)] = e_sums
             nc.scalar.activation(
                 out=e_tile[:, :, x_lo : x_lo + len(blocks) * BLOCK_X, :],
-                in_=live[("s", n, j)][:, : len(blocks)]
+                in_=live[("s", t)][:, : len(blocks)]
                 .rearrange("p g c -> p (g c)")
                 .rearrange("p (x u i) -> p u x i", u=2, i=2),
-                func=ACT.Exp, bias=live[("bias", n, j)][:], scale=SCALE,
-                accum_out=live[("sums", n)][:, j : j + 1],
+                func=ACT.Exp, bias=live[("bias", g)][:, j : j + 1], scale=SCALE,
+                accum_out=live[("sums", g)][:, j : j + 1],
             )
-            live[("e", n, j)] = e_tile
+            live[("e", t)] = e_tile
 
-        def transpose_e(n):
-            eT_ps = psum_2.tile([P, 2, 2, Q_TILE], F32, tag="eT")
-            for j in range(2):
+        def transpose_e(g):
+            tiles = GROUPS[g]
+            eT_ps = psum_2.tile([P, len(tiles), 2, Q_TILE], F32, tag="eT")
+            for j, t in enumerate(tiles):
                 for u in range(2):
-                    words = live[("e", n, j)][:, u].rearrange("p x i -> p (x i)").bitcast(F32)
+                    words = live[("e", t)][:, u].rearrange("p x i -> p (x i)").bitcast(F32)
                     nc.tensor.transpose(eT_ps[:, j, u, :], words, ident_f32[:])
-            live[("eT", n)] = eT_ps
+            live[("eT", g)] = eT_ps
 
-        def regroup_e(n):
+        def regroup_e(g, copy):
+            n = len(GROUPS[g])
             e_grouped = work.tile([P, 2, Q_TILE, PACK], BF16, align_bytes=64)
-            nc.scalar.copy(
-                out=e_grouped[:]
+            copy(
+                out=e_grouped[:, :n]
                 .rearrange("p j i t -> p (j i t)")
                 .bitcast(F32)
-                .rearrange("p (j i u) -> p j i u", j=2, u=2),
-                in_=live[("eT", n)][:].rearrange("p j u i -> p j i u"),
+                .rearrange("p (j i u) -> p j i u", j=n, u=2),
+                in_=live[("eT", g)][:].rearrange("p j u i -> p j i u"),
             )
-            live[("eg", n)] = e_grouped
+            live[("eg", g)] = e_grouped
 
-        def quantise_e(n):
+        def quantise_e(g):
+            n = len(GROUPS[g])
             e_codes = work.tile([P, 2 * Q_TILE], U32, align_bytes=64)
             e_scales = work.tile([P, 2 * Q_TILE], U8, align_bytes=64)
             nc.vector.quantize_mx(
-                out=e_codes[:].bitcast(FP8X4),
-                scales=e_scales[:],
-                in_=live[("eg", n)][:].rearrange("p j i t -> p (j i t)"),
+                out=e_codes[:, : n * Q_TILE].bitcast(FP8X4),
+                scales=e_scales[:, : n * Q_TILE],
+                in_=live[("eg", g)][:, :n].rearrange("p j i t -> p (j i t)"),
             )
-            live[("ec", n)] = (e_codes, e_scales)
+            live[("ec", g)] = (e_codes, e_scales)
 
-        def weighted_sum(n):
-            e_codes, e_scales = live[("ec", n)]
-            o_ps = psum_1.tile([P, 2, DIM], F32, tag="o")
-            live[("o", n)] = o_ps
-            for j in range(2):
+        def weighted_sum(g, pool=psum_1, tag="o"):
+            e_codes, e_scales = live[("ec", g)]
+            o_ps = pool.tile([P, 2, DIM], F32, tag=tag)
+            live[("o", g)] = o_ps
+            for j, t in enumerate(GROUPS[g]):
                 cols = slice(j * Q_TILE, (j + 1) * Q_TILE)
                 nc.tensor.matmul_mx(
                     out=o_ps[:, j, :],
                     lhsT=e_codes[:, cols].bitcast(FP8X4),
                     lhsT_scale=e_scales[:, cols],
-                    rhs=v_codes[:, n, :].bitcast(FP8X4),
-                    rhs_scale=v_scales[:, n, :],
+                    rhs=v_codes[:, span_of(t), :].bitcast(FP8X4),
+                    rhs_scale=v_scales[:, span_of(t), :],
                     start=True,
                     stop=True,
                 )
 
-        def invert_sums(n):
+        def invert_sums(g):
+            n = len(GROUPS[g])
             r_sums = small.tile([P, 2], F32)
-            nc.vector.reciprocal(out=r_sums[:], in_=live[("sums", n)][:])
-            live[("1/sums", n)] = r_sums
+            nc.vector.reciprocal(out=r_sums[:, :n], in_=live[("sums", g)][:, :n])
+            live[("1/sums", g)] = r_sums
 
-        def finish(n):
+        def divide(g):
+            n = len(GROUPS[g])
             o_sb = work.tile([P, 2, DIM], F32)
+            factors = live[("1/sums", g)][:, :n].unsqueeze(2)
             nc.vector.tensor_tensor(
-                out=o_sb[:], in0=live[("o", n)][:],
-                in1=live[("1/sums", n)][:].unsqueeze(2).to_broadcast([P, 2, DIM]), op=ALU.mult,
+                out=o_sb[:, :n], in0=live[("o", g)][:, :n],
+                in1=factors.to_broadcast([P, n, DIM]), op=ALU.mult,
             )
-            row0 = n * 2 * Q_TILE
+            live[("out", g)] = o_sb
+
+        def divide_on_scalar(g):
+            o_sb = work.tile([P, 2, DIM], F32)
+            for j in range(len(GROUPS[g])):
+                nc.scalar.activation(
+                    out=o_sb[:, j, :], in_=live[("o", g)][:, j, :], func=ACT.Copy,
+                    scale=live[("1/sums", g)][:, j : j + 1],
+                )
+            live[("out", g)] = o_sb
+
+        def store(g):
+            n, row0 = len(GROUPS[g]), GROUPS[g][0] * Q_TILE
             nc.sync.dma_start(
-                out=out_rows[row0 : row0 + 2 * Q_TILE, :].rearrange("(j p) d -> p j d", p=P),
-                in_=o_sb[:],
+                out=out_rows[row0 : row0 + n * Q_TILE, :].rearrange("(j p) d -> p j d", p=P),
+                in_=live[("out", g)][:, :n],
             )
 
-        for n in range(FIRST_STEPS):
-            transpose_step(n)
-        for n in range(FIRST_STEPS):
-            keep_step(n)
-        transpose_step(FIRST_STEPS)
+        first_step()
+        scores(0)
+        transpose_step(1)
+        keep_step(1, nc.scalar.copy)
+        regroup_v(0)
+        row_max(0)
+        transpose_step(2)
+        keep_step(2, nc.vector.tensor_copy)
+        scores(1)
+        scores(2)
+        transpose_step(3)
 
-        for i in range(-2, N_PAIRS + 2):
-            before, now, after, later = [0 <= i + d < N_PAIRS for d in (-2, 0, 1, 2)]
-            if before:
-                quantise_e(i - 2)
-            if now:
-                quantise_v(i)
-            if after:
-                regroup_v(i + 1)
-                row_max(i + 1, 0)
-                row_max(i + 1, 1)
-            if 0 <= i - 1 < N_PAIRS:
+        quantised = 0
+        last = N_GROUPS - 1
+        for i in range(N_GROUPS):
+            if i < last:
+                row_max(i + 1)
+            if i >= 1:
                 transpose_e(i - 1)
-            if now:
-                exponentials(i, 0)
-            if later:
-                scores(i + 2, 0)
-            if before:
-                weighted_sum(i - 2)
-            if now:
+            exponentials(i, 0)
+            if i + 2 <= last:
+                scores(GROUPS[i + 2][0])
+            if i >= 3:
+                weighted_sum(i - 3)
+            if 0 < i < last:
                 exponentials(i, 1)
-            if later:
-                scores(i + 2, 1)
-            if i + STEPS_AHEAD < N_STEPS:
-                keep_step(i + STEPS_AHEAD)
-            if 0 <= i - 1 < N_PAIRS:
-                regroup_e(i - 1)
-            if before:
-                invert_sums(i - 2)
-                finish(i - 2)
-            if i + STEPS_AHEAD + 1 < N_STEPS:
-                transpose_step(i + STEPS_AHEAD + 1)
+            if i + 2 < last:
+                scores(GROUPS[i + 2][1])
+            if i + 3 < N_STEPS:
+                keep_step(i + 3, nc.scalar.copy)
+            if i >= 1:
+                regroup_e(i - 1, nc.scalar.copy)
+            if i >= 3:
+                invert_sums(i - 3)
+                divide(i - 3)
+                store(i - 3)
+            if i >= 2:
+                quantise_e(i - 2)
+            if quantised <= span_of(GROUPS[i][-1]):
+                quantise_v(quantised)
+                quantised += 1
+                if quantised < HEADS * SPANS:
+                    regroup_v(quantised)
+            if i + 4 < N_STEPS:
+                transpose_step(i + 4)
+
+        invert_sums(last - 2)
+        transpose_e(last)
+        weighted_sum(last - 2)
+        regroup_e(last, nc.vector.tensor_copy)
+        quantise_e(last - 1)
+        divide_on_scalar(last - 2)
+        store(last - 2)
+        weighted_sum(last - 1, psum_s, "s")
+        quantise_e(last)
+        weighted_sum(last, psum_s, "s")
+        invert_sums(last - 1)
+        invert_sums(last)
+        divide(last - 1)
+        store(last - 1)
+        divide_on_scalar(last)
+        store(last)

@@ -201,7 +201,8 @@ def tile_sparseattention_kernel(tc, q, k, v, out):
                     start=True, stop=True,
                 )
                 return
-            for g, b in enumerate(key_blocks(t)):
+            blocks = key_blocks(t)
+            for g, b in sorted(enumerate(blocks), key=lambda pair: pair[1] == t):
                 if b != t:
                     nc.tensor.matmul(
                         s_ps[:, g, :], lhsT=triT[:, 0 if b < t else 1, :], rhs=ident_f32[:],
@@ -216,16 +217,19 @@ def tile_sparseattention_kernel(tc, q, k, v, out):
             tiles = GROUPS[g]
             least = small.tile([P, 2], F32)
             bias = small.tile([P, 2], F32)
+            scaled = 0
             for j, t in enumerate(tiles):
                 nc.vector.tensor_reduce(
                     out=least[:, j : j + 1],
                     in_=live[("s", t)][:, : len(key_blocks(t))].rearrange("p g c -> p (g c)"),
                     axis=AXIS.X, op=ALU.max, negate=True,
                 )
-            nc.gpsimd.tensor_scalar(
-                out=bias[:, : len(tiles)], in0=least[:, : len(tiles)],
-                scalar1=SCALE, scalar2=0.0, op0=ALU.mult, op1=ALU.add,
-            )
+                if g < 2 or j == len(tiles) - 1:
+                    nc.gpsimd.tensor_scalar(
+                        out=bias[:, scaled : j + 1], in0=least[:, scaled : j + 1],
+                        scalar1=SCALE, scalar2=0.0, op0=ALU.mult, op1=ALU.add,
+                    )
+                    scaled = j + 1
             live[("bias", g)] = bias
 
         def exponentials(g, j):
@@ -304,7 +308,7 @@ def tile_sparseattention_kernel(tc, q, k, v, out):
 
         def divide(g):
             n = len(GROUPS[g])
-            o_sb = work.tile([P, 2, DIM], F32)
+            o_sb = work.tile([P, 2, DIM], F32, bufs=4)
             factors = live[("1/sums", g)][:, :n].unsqueeze(2)
             nc.vector.tensor_tensor(
                 out=o_sb[:, :n], in0=live[("o", g)][:, :n],
@@ -313,7 +317,7 @@ def tile_sparseattention_kernel(tc, q, k, v, out):
             live[("out", g)] = o_sb
 
         def divide_on_scalar(g):
-            o_sb = work.tile([P, 2, DIM], F32)
+            o_sb = work.tile([P, 2, DIM], F32, bufs=4)
             for j in range(len(GROUPS[g])):
                 nc.scalar.activation(
                     out=o_sb[:, j, :], in_=live[("o", g)][:, j, :], func=ACT.Copy,
@@ -329,11 +333,11 @@ def tile_sparseattention_kernel(tc, q, k, v, out):
             )
 
         first_step()
-        scores(0)
         transpose_step(1)
         keep_step(1, nc.scalar.copy)
-        regroup_v(0)
+        scores(0)
         row_max(0)
+        regroup_v(0)
         transpose_step(2)
         keep_step(2, nc.vector.tensor_copy)
         scores(1)
@@ -374,18 +378,18 @@ def tile_sparseattention_kernel(tc, q, k, v, out):
             if i + 4 < N_STEPS:
                 transpose_step(i + 4)
 
-        invert_sums(last - 2)
         transpose_e(last)
-        weighted_sum(last - 2)
-        regroup_e(last, nc.vector.tensor_copy)
-        quantise_e(last - 1)
-        divide_on_scalar(last - 2)
-        store(last - 2)
-        weighted_sum(last - 1, psum_s, "s")
-        quantise_e(last)
-        weighted_sum(last, psum_s, "s")
+        weighted_sum(last - 2, psum_s, "s")
+        regroup_e(last, nc.scalar.copy)
+        invert_sums(last - 2)
         invert_sums(last - 1)
         invert_sums(last)
+        quantise_e(last - 1)
+        weighted_sum(last - 1, psum_s, "s")
+        divide_on_scalar(last - 2)
+        store(last - 2)
+        quantise_e(last)
+        weighted_sum(last, psum_s, "s")
         divide(last - 1)
         store(last - 1)
         divide_on_scalar(last)

@@ -365,10 +365,10 @@ def tile_sparseattention_kernel(tc, q, k, v, out):
             if i >= 1:
                 regroup_e(i - 1, nc.scalar.copy)
             if i >= 3:
-                invert_sums(i - 3)
                 divide(i - 3)
                 store(i - 3)
             if i >= 2:
+                invert_sums(i - 2)
                 quantise_e(i - 2)
             if quantised <= span_of(GROUPS[i][-1]):
                 quantise_v(quantised)
@@ -381,7 +381,6 @@ def tile_sparseattention_kernel(tc, q, k, v, out):
         transpose_e(last)
         weighted_sum(last - 2, psum_s, "s")
         regroup_e(last, nc.scalar.copy)
-        invert_sums(last - 2)
         invert_sums(last - 1)
         invert_sums(last)
         quantise_e(last - 1)

@@ -25,13 +25,13 @@ STEP = 2
 N_STEPS = BLOCKS // STEP
 BLOCK = 128
 BLOCK_X = BLOCK // PACK
-EDGE_TILES = 2
+MASK_STEP = 4
 SCALE = 1.0 / DIM**0.5
 MASKED = -1.0e30
 
 FLOPS = 2 * 2 * HEADS * SEQ * SPAN * DIM
 
-HEAD_STEPS = 2
+HEAD_STEPS = 4
 SPANS = (TILES - 2) // 2
 GROUPS = [[0]] + [[t, t + 1] for t in range(1, BLOCKS - 1, 2)] + [[BLOCKS - 1]]
 N_GROUPS = len(GROUPS)
@@ -187,7 +187,9 @@ def tile_sparseattention_kernel(tc, q, k, v, out):
             s_ps = psum_s.tile([P, 3, BLOCK], F32, tag="s")
             live[("s", t)] = s_ps
             queries = kqT[:, t // STEP, STEP + t % STEP, :]
-            if EDGE_TILES <= t % TILES < TILES - EDGE_TILES:
+            blocks = key_blocks(t)
+            by_transpose = len(blocks) == 3 and t % MASK_STEP == MASK_STEP - 1
+            if len(blocks) == 3 and not by_transpose:
                 nc.tensor.matmul(
                     s_ps[:, 0:3:2, :], lhsT=ident[:], rhs=tri[:], start=True, stop=False
                 )
@@ -201,12 +203,16 @@ def tile_sparseattention_kernel(tc, q, k, v, out):
                     start=True, stop=True,
                 )
                 return
-            blocks = key_blocks(t)
             for g, b in sorted(enumerate(blocks), key=lambda pair: pair[1] == t):
-                if b != t:
+                side = 0 if b < t else 1
+                if b != t and by_transpose:
                     nc.tensor.matmul(
-                        s_ps[:, g, :], lhsT=triT[:, 0 if b < t else 1, :], rhs=ident_f32[:],
+                        s_ps[:, g, :], lhsT=triT[:, side, :], rhs=ident_f32[:],
                         is_transpose=True, start=True, stop=False,
+                    )
+                elif b != t:
+                    nc.tensor.matmul(
+                        s_ps[:, g, :], lhsT=ident[:], rhs=tri[:, side, :], start=True, stop=False
                     )
                 nc.tensor.matmul(
                     s_ps[:, g, :], lhsT=queries, rhs=kqT[:, b // STEP, b % STEP, :],
@@ -337,7 +343,6 @@ def tile_sparseattention_kernel(tc, q, k, v, out):
         keep_step(1, nc.scalar.copy)
         scores(0)
         row_max(0)
-        regroup_v(0)
         transpose_step(2)
         keep_step(2, nc.vector.tensor_copy)
         scores(1)
@@ -349,17 +354,13 @@ def tile_sparseattention_kernel(tc, q, k, v, out):
         for i in range(N_GROUPS):
             if i < last:
                 row_max(i + 1)
-            if i >= 1:
-                transpose_e(i - 1)
-            exponentials(i, 0)
-            if i + 2 <= last:
-                scores(GROUPS[i + 2][0])
+            for j in range(len(GROUPS[i])):
+                exponentials(i, j)
             if i >= 3:
                 weighted_sum(i - 3)
-            if 0 < i < last:
-                exponentials(i, 1)
-            if i + 2 < last:
-                scores(GROUPS[i + 2][1])
+            if i + 2 <= last:
+                for t in GROUPS[i + 2]:
+                    scores(t)
             if i + 3 < N_STEPS:
                 keep_step(i + 3, nc.scalar.copy)
             if i >= 1:
@@ -370,15 +371,17 @@ def tile_sparseattention_kernel(tc, q, k, v, out):
             if i >= 2:
                 invert_sums(i - 2)
                 quantise_e(i - 2)
-            if quantised <= span_of(GROUPS[i][-1]):
+            if i == 0:
+                regroup_v(0)
+            elif quantised <= span_of(GROUPS[i - 1][-1]):
                 quantise_v(quantised)
                 quantised += 1
                 if quantised < HEADS * SPANS:
                     regroup_v(quantised)
             if i + 4 < N_STEPS:
                 transpose_step(i + 4)
+            transpose_e(i)
 
-        transpose_e(last)
         weighted_sum(last - 2, psum_s, "s")
         regroup_e(last, nc.scalar.copy)
         invert_sums(last - 1)

@@ -32,6 +32,7 @@ MASKED = -1.0e30
 FLOPS = 2 * 2 * HEADS * SEQ * SPAN * DIM
 
 HEAD_STEPS = 4
+WARM_UPS = 12
 SPANS = (TILES - 2) // 2
 GROUPS = [[0]] + [[t, t + 1] for t in range(1, BLOCKS - 1, 2)] + [[BLOCKS - 1]]
 N_GROUPS = len(GROUPS)
@@ -94,8 +95,26 @@ def tile_sparseattention_kernel(tc, q, k, v, out):
                 load_span(loaded)
                 loaded += 1
 
+        zeros = keep.tile([P, P * PACK], BF16, align_bytes=64)
+        zero_codes = keep.tile([P, P], U32, align_bytes=64)
+        zero_scales = keep.tile([P, P], U8, align_bytes=64)
+        nc.vector.memset(zeros[:].bitcast(U32), 0)
+        nc.vector.quantize_mx(
+            out=zero_codes[:].bitcast(FP8X4), scales=zero_scales[:], in_=zeros[:]
+        )
         ident = keep.tile([P, P], BF16)
         make_identity(nc, ident[:])
+        tri = keep.tile([P, 2, P], BF16)
+        nc.gpsimd.memset(tri[:], 0.0)
+        nc.gpsimd.affine_select(
+            out=tri[:, 0, :], in_=tri[:, 0, :], pattern=[[1, P]],
+            compare_op=ALU.is_ge, fill=MASKED, base=0, channel_multiplier=-1,
+        )
+        nc.gpsimd.affine_select(
+            out=tri[:, 1, :], in_=tri[:, 1, :], pattern=[[-1, P]],
+            compare_op=ALU.is_ge, fill=MASKED, base=-1, channel_multiplier=1,
+        )
+
         ident_f32 = keep.tile([P, P], F32)
         make_identity(nc, ident_f32[:])
 
@@ -108,17 +127,6 @@ def tile_sparseattention_kernel(tc, q, k, v, out):
         nc.gpsimd.affine_select(
             out=triT[:, 1, :], in_=triT[:, 1, :], pattern=[[1, P]],
             compare_op=ALU.is_ge, fill=MASKED, base=-1, channel_multiplier=-1,
-        )
-
-        tri = keep.tile([P, 2, P], BF16)
-        nc.gpsimd.memset(tri[:], 0.0)
-        nc.gpsimd.affine_select(
-            out=tri[:, 0, :], in_=tri[:, 0, :], pattern=[[1, P]],
-            compare_op=ALU.is_ge, fill=MASKED, base=0, channel_multiplier=-1,
-        )
-        nc.gpsimd.affine_select(
-            out=tri[:, 1, :], in_=tri[:, 1, :], pattern=[[-1, P]],
-            compare_op=ALU.is_ge, fill=MASKED, base=-1, channel_multiplier=1,
         )
 
         E_BUFS = 2
@@ -314,7 +322,7 @@ def tile_sparseattention_kernel(tc, q, k, v, out):
 
         def divide(g):
             n = len(GROUPS[g])
-            o_sb = work.tile([P, 2, DIM], F32, bufs=4)
+            o_sb = work.tile([P, 2, DIM], F32, bufs=6)
             factors = live[("1/sums", g)][:, :n].unsqueeze(2)
             nc.vector.tensor_tensor(
                 out=o_sb[:, :n], in0=live[("o", g)][:, :n],
@@ -323,7 +331,7 @@ def tile_sparseattention_kernel(tc, q, k, v, out):
             live[("out", g)] = o_sb
 
         def divide_on_scalar(g):
-            o_sb = work.tile([P, 2, DIM], F32, bufs=4)
+            o_sb = work.tile([P, 2, DIM], F32, bufs=6)
             for j in range(len(GROUPS[g])):
                 nc.scalar.activation(
                     out=o_sb[:, j, :], in_=live[("o", g)][:, j, :], func=ACT.Copy,
@@ -336,6 +344,15 @@ def tile_sparseattention_kernel(tc, q, k, v, out):
             nc.sync.dma_start(
                 out=out_rows[row0 : row0 + n * Q_TILE, :].rearrange("(j p) d -> p j d", p=P),
                 in_=live[("out", g)][:, :n],
+            )
+
+        warm_ps = psum_s.tile([P, P], F32, tag="s")
+        for n in range(WARM_UPS):
+            nc.tensor.matmul_mx(
+                out=warm_ps[:],
+                lhsT=zero_codes[:].bitcast(FP8X4), lhsT_scale=zero_scales[:],
+                rhs=zero_codes[:].bitcast(FP8X4), rhs_scale=zero_scales[:],
+                start=True, stop=True,
             )
 
         first_step()
@@ -352,22 +369,23 @@ def tile_sparseattention_kernel(tc, q, k, v, out):
         quantised = 0
         last = N_GROUPS - 1
         for i in range(N_GROUPS):
+            if i >= 4:
+                divide(i - 4)
+                store(i - 4)
             if i < last:
                 row_max(i + 1)
             for j in range(len(GROUPS[i])):
                 exponentials(i, j)
+            if i + 2 <= last:
+                scores(GROUPS[i + 2][0])
             if i >= 3:
                 weighted_sum(i - 3)
-            if i + 2 <= last:
-                for t in GROUPS[i + 2]:
-                    scores(t)
+            if i + 2 < last:
+                scores(GROUPS[i + 2][1])
             if i + 3 < N_STEPS:
                 keep_step(i + 3, nc.scalar.copy)
             if i >= 1:
                 regroup_e(i - 1, nc.scalar.copy)
-            if i >= 3:
-                divide(i - 3)
-                store(i - 3)
             if i >= 2:
                 invert_sums(i - 2)
                 quantise_e(i - 2)
@@ -383,6 +401,8 @@ def tile_sparseattention_kernel(tc, q, k, v, out):
             transpose_e(i)
 
         weighted_sum(last - 2, psum_s, "s")
+        divide(last - 3)
+        store(last - 3)
         regroup_e(last, nc.scalar.copy)
         invert_sums(last - 1)
         invert_sums(last)

from contextlib import ExitStack

import concourse.mybir as mybir
from concourse.masks import make_identity

BF16 = mybir.dt.bfloat16
F32 = mybir.dt.float32
U32 = mybir.dt.uint32
U8 = mybir.dt.uint8
FP8X4 = mybir.dt.float8_e4m3fn_x4
ALU = mybir.AluOpType
ACT = mybir.ActivationFunctionType
AXIS = mybir.AxisListType

P = 128
PACK = 4
HEADS = 2
SEQ = 2048
DIM = 128
SPAN = P * PACK
Q_TILE = P
TILES = SEQ // Q_TILE
BLOCKS = HEADS * TILES
STEP = 2
N_STEPS = BLOCKS // STEP
BLOCK = 128
BLOCK_X = BLOCK // PACK
MASK_STEP = 4
SCALE = 1.0 / DIM**0.5
MASKED = -1.0e30

FLOPS = 2 * 2 * HEADS * SEQ * SPAN * DIM

HEAD_STEPS = 4
WARM_UPS = 12
SPANS = (TILES - 2) // 2
GROUPS = [[0]] + [[t, t + 1] for t in range(1, BLOCKS - 1, 2)] + [[BLOCKS - 1]]
N_GROUPS = len(GROUPS)


def span_of(t):
    return SPANS * (t // TILES) + min(max((t % TILES - 1) // 2, 0), SPANS - 1)


def span_block(span):
    return (span // SPANS) * TILES + 2 * (span % SPANS)


def key_blocks(t):
    return [b for b in (t - 1, t, t + 1) if 0 <= b < BLOCKS and b // TILES == t // TILES]


def tile_sparseattention_kernel(tc, q, k, v, out):
    nc = tc.nc
    q_rows = q.rearrange("b h s d -> (b h s) d")
    k_rows = k.rearrange("b h s d -> (b h s) d")
    v_rows = v.rearrange("b h s d -> (b h s) d")
    out_rows = out.rearrange("b h s d -> (b h s) d")

    with ExitStack() as ctx:
        keep = ctx.enter_context(tc.tile_pool(name="keep", bufs=1))
        work = ctx.enter_context(tc.tile_pool(name="work", bufs=3))
        small = ctx.enter_context(tc.tile_pool(name="small", bufs=4))
        psum_s = ctx.enter_context(tc.psum_pool(name="psum_s", bufs=4))
        psum_2 = ctx.enter_context(tc.psum_pool(name="psum_2", bufs=2))
        psum_1 = ctx.enter_context(tc.psum_pool(name="psum_1", bufs=1))
        ctx.enter_context(tc.manual_schedule())

        k_raw = keep.tile([P, BLOCKS, DIM], BF16)
        q_raw = keep.tile([P, BLOCKS, DIM], BF16)
        v_raw = keep.tile([P, HEADS * SPANS, PACK, DIM], BF16)

        def load_steps(first, last):
            blocks = slice(first * STEP, last * STEP)
            rows = slice(first * STEP * BLOCK, last * STEP * BLOCK)
            for raw, dram in ((k_raw, k_rows), (q_raw, q_rows)):
                nc.sync.dma_start(
                    out=raw[:, blocks, :], in_=dram[rows, :].rearrange("(b p) d -> p b d", p=P)
                )

        def load_span(span):
            c = span_block(span) * BLOCK
            nc.sync.dma_start(
                out=v_raw[:, span].rearrange("p t d -> p (t d)"),
                in_=v_rows[c : c + SPAN, :].rearrange("(p t) d -> p (t d)", t=PACK),
            )

        for first in range(HEAD_STEPS):
            load_steps(first, first + 1)
        loaded = 0
        for first in range(HEAD_STEPS, N_STEPS + STEP, 2):
            if first < N_STEPS:
                load_steps(first, first + 2)
            while loaded < HEADS * SPANS and loaded <= span_of(GROUPS[first - 1][-1]):
                load_span(loaded)
                loaded += 1

        zeros = keep.tile([P, P * PACK], BF16, align_bytes=64)
        zero_codes = keep.tile([P, P], U32, align_bytes=64)
        zero_scales = keep.tile([P, P], U8, align_bytes=64)
        nc.vector.memset(zeros[:].bitcast(U32), 0)
        nc.vector.quantize_mx(
            out=zero_codes[:].bitcast(FP8X4), scales=zero_scales[:], in_=zeros[:]
        )
        ident = keep.tile([P, P], BF16)
        make_identity(nc, ident[:])
        tri = keep.tile([P, 2, P], BF16)
        nc.gpsimd.memset(tri[:], 0.0)
        nc.gpsimd.affine_select(
            out=tri[:, 0, :], in_=tri[:, 0, :], pattern=[[1, P]],
            compare_op=ALU.is_ge, fill=MASKED, base=0, channel_multiplier=-1,
        )
        nc.gpsimd.affine_select(
            out=tri[:, 1, :], in_=tri[:, 1, :], pattern=[[-1, P]],
            compare_op=ALU.is_ge, fill=MASKED, base=-1, channel_multiplier=1,
        )

        ident_f32 = keep.tile([P, P], F32)
        make_identity(nc, ident_f32[:])

        triT = keep.tile([P, 2, P], F32)
        nc.gpsimd.memset(triT[:], 0.0)
        nc.gpsimd.affine_select(
            out=triT[:, 0, :], in_=triT[:, 0, :], pattern=[[-1, P]],
            compare_op=ALU.is_ge, fill=MASKED, base=0, channel_multiplier=1,
        )
        nc.gpsimd.affine_select(
            out=triT[:, 1, :], in_=triT[:, 1, :], pattern=[[1, P]],
            compare_op=ALU.is_ge, fill=MASKED, base=-1, channel_multiplier=-1,
        )

        E_BUFS = 2
        e_tiles = {}
        e_uses = {}
        for case in ((0, 2), (0, 3), (BLOCK_X, 3), (2 * BLOCK_X, 2)):
            e_uses[case] = 0
            for b in range(E_BUFS):
                e_tile = keep.tile([P, 2, P, 2], BF16, name="e%d_%d_%d" % (case[0], case[1], b))
                seen = (case[0], case[0] + case[1] * BLOCK_X)
                for lo, hi in ((0, seen[0]), (seen[1], P)):
                    if lo < hi:
                        nc.vector.memset(e_tile[:, :, lo:hi, :], 0.0)
                e_tiles[(case, b)] = e_tile

        kqT = keep.tile([P, N_STEPS, 2 * STEP, BLOCK], BF16)
        live = {}

        def transpose_step(s):
            t_ps = psum_1.tile([P, 2 * STEP, P], BF16, tag="o" if s == 2 else "tp")
            for b in range(STEP):
                nc.tensor.transpose(t_ps[:, b, :], k_raw[:, s * STEP + b, :], ident[:])
            for b in range(STEP):
                nc.tensor.transpose(t_ps[:, STEP + b, :], q_raw[:, s * STEP + b, :], ident[:])
            live[("step", s)] = t_ps

        def keep_step(s, copy):
            copy(
                out=kqT[:, s].rearrange("p b i -> p (b i)").bitcast(F32),
                in_=live[("step", s)][:].rearrange("p b i -> p (b i)").bitcast(F32),
            )

        def first_step():
            k_ps = psum_2.tile([P, STEP, P], BF16, tag="eT")
            q_ps = psum_2.tile([P, STEP, P], BF16, tag="eT")
            for t_ps, raw in ((k_ps, k_raw), (q_ps, q_raw)):
                for b in range(STEP):
                    nc.tensor.transpose(t_ps[:, b, :], raw[:, b, :], ident[:])
            for t_ps, copy, lo in (
                (k_ps, nc.vector.tensor_copy, 0),
                (q_ps, nc.scalar.copy, STEP),
            ):
                copy(
                    out=kqT[:, 0, lo : lo + STEP].rearrange("p b i -> p (b i)").bitcast(F32),
                    in_=t_ps[:].rearrange("p b i -> p (b i)").bitcast(F32),
                )

        v_codes = keep.tile([P, HEADS * SPANS, DIM], U32, align_bytes=64)
        v_scales = keep.tile([P, HEADS * SPANS, DIM], U8, align_bytes=64)
        v_grouped = keep.tile([P, DIM, PACK], BF16, align_bytes=64)

        def regroup_v(span):
            nc.gpsimd.tensor_scalar(
                out=v_grouped[:], in0=v_raw[:, span].rearrange("p t d -> p d t"),
                scalar1=1.0, scalar2=0.0, op0=ALU.mult, op1=ALU.add,
            )

        def quantise_v(span):
            nc.vector.quantize_mx(
                out=v_codes[:, span, :].bitcast(FP8X4),
                scales=v_scales[:, span, :],
                in_=v_grouped[:].rearrange("p d t -> p (d t)"),
            )

        def scores(t):
            s_ps = psum_s.tile([P, 3, BLOCK], F32, tag="s")
            live[("s", t)] = s_ps
            queries = kqT[:, t // STEP, STEP + t % STEP, :]
            blocks = key_blocks(t)
            by_transpose = len(blocks) == 3 and t % MASK_STEP == MASK_STEP - 1
            if len(blocks) == 3 and not by_transpose:
                nc.tensor.matmul(
                    s_ps[:, 0:3:2, :], lhsT=ident[:], rhs=tri[:], start=True, stop=False
                )
                before = (t - 1) // STEP
                nc.tensor.matmul(
                    s_ps[:, 0:3:2, :], lhsT=queries,
                    rhs=kqT[:, before : before + 2, (t - 1) % STEP, :], start=False, stop=True,
                )
                nc.tensor.matmul(
                    s_ps[:, 1, :], lhsT=queries, rhs=kqT[:, t // STEP, t % STEP, :],
                    start=True, stop=True,
                )
                return
            for g, b in sorted(enumerate(blocks), key=lambda pair: pair[1] == t):
                side = 0 if b < t else 1
                if b != t and by_transpose:
                    nc.tensor.matmul(
                        s_ps[:, g, :], lhsT=triT[:, side, :], rhs=ident_f32[:],
                        is_transpose=True, start=True, stop=False,
                    )
                elif b != t:
                    nc.tensor.matmul(
                        s_ps[:, g, :], lhsT=ident[:], rhs=tri[:, side, :], start=True, stop=False
                    )
                nc.tensor.matmul(
                    s_ps[:, g, :], lhsT=queries, rhs=kqT[:, b // STEP, b % STEP, :],
                    start=(b == t), stop=True,
                )

        def row_max(g):
            tiles = GROUPS[g]
            least = small.tile([P, 2], F32)
            bias = small.tile([P, 2], F32)
            scaled = 0
            for j, t in enumerate(tiles):
                nc.vector.tensor_reduce(
                    out=least[:, j : j + 1],
                    in_=live[("s", t)][:, : len(key_blocks(t))].rearrange("p g c -> p (g c)"),
                    axis=AXIS.X, op=ALU.max, negate=True,
                )
                if g < 2 or j == len(tiles) - 1:
                    nc.gpsimd.tensor_scalar(
                        out=bias[:, scaled : j + 1], in0=least[:, scaled : j + 1],
                        scalar1=SCALE, scalar2=0.0, op0=ALU.mult, op1=ALU.add,
                    )
                    scaled = j + 1
            live[("bias", g)] = bias

        def exponentials(g, j):
            t = GROUPS[g][j]
            blocks = key_blocks(t)
            x_lo = (blocks[0] - span_block(span_of(t))) * BLOCK_X
            case = (x_lo, len(blocks))
            e_tile = e_tiles[(case, e_uses[case] % E_BUFS)]
            e_uses[case] += 1
            if j == 0:
                e_sums = small.tile([P, 2], F32)
                live[("sums", g)] = e_sums
            nc.scalar.activation(
                out=e_tile[:, :, x_lo : x_lo + len(blocks) * BLOCK_X, :],
                in_=live[("s", t)][:, : len(blocks)]
                .rearrange("p g c -> p (g c)")
                .rearrange("p (x u i) -> p u x i", u=2, i=2),
                func=ACT.Exp, bias=live[("bias", g)][:, j : j + 1], scale=SCALE,
                accum_out=live[("sums", g)][:, j : j + 1],
            )
            live[("e", t)] = e_tile

        def transpose_e(g):
            tiles = GROUPS[g]
            eT_ps = psum_2.tile([P, len(tiles), 2, Q_TILE], F32, tag="eT")
            for j, t in enumerate(tiles):
                for u in range(2):
                    words = live[("e", t)][:, u].rearrange("p x i -> p (x i)").bitcast(F32)
                    nc.tensor.transpose(eT_ps[:, j, u, :], words, ident_f32[:])
            live[("eT", g)] = eT_ps

        def regroup_e(g, copy):
            n = len(GROUPS[g])
            e_grouped = work.tile([P, 2, Q_TILE, PACK], BF16, align_bytes=64)
            copy(
                out=e_grouped[:, :n]
                .rearrange("p j i t -> p (j i t)")
                .bitcast(F32)
                .rearrange("p (j i u) -> p j i u", j=n, u=2),
                in_=live[("eT", g)][:].rearrange("p j u i -> p j i u"),
            )
            live[("eg", g)] = e_grouped

        def quantise_e(g):
            n = len(GROUPS[g])
            e_codes = work.tile([P, 2 * Q_TILE], U32, align_bytes=64)
            e_scales = work.tile([P, 2 * Q_TILE], U8, align_bytes=64)
            nc.vector.quantize_mx(
                out=e_codes[:, : n * Q_TILE].bitcast(FP8X4),
                scales=e_scales[:, : n * Q_TILE],
                in_=live[("eg", g)][:, :n].rearrange("p j i t -> p (j i t)"),
            )
            live[("ec", g)] = (e_codes, e_scales)

        def weighted_sum(g, pool=psum_1, tag="o"):
            e_codes, e_scales = live[("ec", g)]
            o_ps = pool.tile([P, 2, DIM], F32, tag=tag)
            live[("o", g)] = o_ps
            for j, t in enumerate(GROUPS[g]):
                cols = slice(j * Q_TILE, (j + 1) * Q_TILE)
                nc.tensor.matmul_mx(
                    out=o_ps[:, j, :],
                    lhsT=e_codes[:, cols].bitcast(FP8X4),
                    lhsT_scale=e_scales[:, cols],
                    rhs=v_codes[:, span_of(t), :].bitcast(FP8X4),
                    rhs_scale=v_scales[:, span_of(t), :],
                    start=True,
                    stop=True,
                )

        def invert_sums(g):
            n = len(GROUPS[g])
            r_sums = small.tile([P, 2], F32)
            nc.vector.reciprocal(out=r_sums[:, :n], in_=live[("sums", g)][:, :n])
            live[("1/sums", g)] = r_sums

        def divide(g):
            n = len(GROUPS[g])
            o_sb = work.tile([P, 2, DIM], F32, bufs=6)
            factors = live[("1/sums", g)][:, :n].unsqueeze(2)
            nc.vector.tensor_tensor(
                out=o_sb[:, :n], in0=live[("o", g)][:, :n],
                in1=factors.to_broadcast([P, n, DIM]), op=ALU.mult,
            )
            live[("out", g)] = o_sb

        def divide_on_scalar(g):
            o_sb = work.tile([P, 2, DIM], F32, bufs=6)
            for j in range(len(GROUPS[g])):
                nc.scalar.activation(
                    out=o_sb[:, j, :], in_=live[("o", g)][:, j, :], func=ACT.Copy,
                    scale=live[("1/sums", g)][:, j : j + 1],
                )
            live[("out", g)] = o_sb

        def store(g):
            n, row0 = len(GROUPS[g]), GROUPS[g][0] * Q_TILE
            nc.sync.dma_start(
                out=out_rows[row0 : row0 + n * Q_TILE, :].rearrange("(j p) d -> p j d", p=P),
                in_=live[("out", g)][:, :n],
            )

        warm_ps = psum_s.tile([P, P], F32, tag="s")
        for n in range(WARM_UPS):
            nc.tensor.matmul_mx(
                out=warm_ps[:],
                lhsT=zero_codes[:].bitcast(FP8X4), lhsT_scale=zero_scales[:],
                rhs=zero_codes[:].bitcast(FP8X4), rhs_scale=zero_scales[:],
                start=True, stop=True,
            )

        first_step()
        transpose_step(1)
        keep_step(1, nc.scalar.copy)
        scores(0)
        row_max(0)
        transpose_step(2)
        keep_step(2, nc.vector.tensor_copy)
        scores(1)
        scores(2)
        transpose_step(3)

        quantised = 0
        last = N_GROUPS - 1
        for i in range(N_GROUPS):
            if i >= 4:
                divide(i - 4)
                store(i - 4)
            if i < last:
                row_max(i + 1)
            for j in range(len(GROUPS[i])):
                exponentials(i, j)
            if i + 2 <= last:
                scores(GROUPS[i + 2][0])
            if i >= 3:
                weighted_sum(i - 3)
            if i + 2 < last:
                scores(GROUPS[i + 2][1])
            if i + 3 < N_STEPS:
                keep_step(i + 3, nc.scalar.copy)
            if i >= 1:
                regroup_e(i - 1, nc.scalar.copy)
            if i >= 2:
                invert_sums(i - 2)
                quantise_e(i - 2)
            if i == 0:
                regroup_v(0)
            elif quantised <= span_of(GROUPS[i - 1][-1]):
                quantise_v(quantised)
                quantised += 1
                if quantised < HEADS * SPANS:
                    regroup_v(quantised)
            if i + 4 < N_STEPS:
                transpose_step(i + 4)
            transpose_e(i)

        weighted_sum(last - 2, psum_s, "s")
        divide(last - 3)
        store(last - 3)
        regroup_e(last, nc.scalar.copy)
        invert_sums(last - 1)
        invert_sums(last)
        quantise_e(last - 1)
        weighted_sum(last - 1, psum_s, "s")
        divide_on_scalar(last - 2)
        store(last - 2)
        quantise_e(last)
        weighted_sum(last, psum_s, "s")
        divide(last - 1)
        store(last - 1)
        divide_on_scalar(last)
        store(last)
